import numpy as np
import ml_dtypes


def mxq(x, axis, fmt="e4m3"):
    dtype, down = {"e4m3": (ml_dtypes.float8_e4m3fn, 7), "e5m2": (ml_dtypes.float8_e5m2, 14)}[fmt]
    v = np.moveaxis(np.asarray(x, np.float32).astype(ml_dtypes.bfloat16).astype(np.float64), axis, -1)
    blocks = v.reshape(v.shape[:-1] + (-1, 32))
    amax = np.abs(blocks).max(-1, keepdims=True)
    byte = np.maximum(np.where(amax > 0, np.frexp(amax)[1] - 1 + 127, 0) - down, 1)
    scale = np.exp2(byte - 127.0)
    codes = (blocks / scale).astype(np.float32).astype(dtype).astype(np.float64)
    return np.moveaxis((codes * scale).reshape(v.shape), -1, axis)


WIDE = False


def mx_kscale(k):
    if not WIDE:
        return np.ones(k)
    levels = np.array([10, -10, 5, -5, 0])
    a = np.random.permutation(np.resize(levels, k // 512 * 4)).reshape(k // 512, 4)
    idx = np.arange(k)
    return np.exp2(a[idx // 512, idx % 128 // 32])


BF16 = ml_dtypes.bfloat16


def bf(x):
    return np.asarray(x, np.float32).astype(BF16)


def f64(x):
    return np.asarray(x).astype(np.float64)


E2M1 = np.array([0.0, 0.5, 1.0, 1.5, 2.0, 3.0, 4.0, 6.0, -0.0, -0.5, -1.0, -1.5, -2.0, -3.0, -4.0, -6.0])


def pack_weight(w, fmt):
    k, n = w.shape
    w = f64(bf(w)).reshape(k // 32, 32, n)
    amax = np.abs(w).max(1)
    if fmt == "e4m3":
        byte = np.frexp(amax)[1] - 1 + 127 - 7
    else:
        mant, ex = np.frexp(amax / 6.0)
        byte = np.where(mant > 0.5, ex, ex - 1) + 127
    byte = np.clip(np.where(amax > 0, byte, 1), 1, 254)
    scaled = (w * np.exp2(127.0 - byte)[:, None, :]).reshape(k, n).astype(np.float32)
    by_word = np.ascontiguousarray(scaled.reshape(k // 512, 128, 4, n).transpose(0, 1, 3, 2))
    if fmt == "e4m3":
        words = by_word.astype(ml_dtypes.float8_e4m3fn).view(np.uint8)
    else:
        c = by_word.astype(ml_dtypes.float4_e2m1fn).view(np.uint8) & 0xF
        words = c[..., 0::2] | (c[..., 1::2] << 4)
    return np.ascontiguousarray(words), np.ascontiguousarray(byte.astype(np.uint8).reshape(k // 512, 16, n))


def unpack_weight(words, scales, fmt):
    g, p, n, _ = words.shape
    if fmt == "e4m3":
        vals = np.ascontiguousarray(words).view(ml_dtypes.float8_e4m3fn).astype(np.float64)
    else:
        nib = np.empty((g, p, n, 4), np.uint8)
        nib[..., 0::2] = words & 0xF
        nib[..., 1::2] = words >> 4
        vals = E2M1[nib]
    vals = vals * np.repeat(np.exp2(scales.astype(np.float64) - 127.0), 8, axis=1)[..., None]
    return vals.transpose(0, 1, 3, 2).reshape(g * 512, n)


E, D, H, C = 128, 2048, 4096, 128


def silu(v):
    return v / (1.0 + np.exp(-v))


def setup_inputs():
    s = mx_kscale(D)
    t = mx_kscale(H)
    node_embed = bf(np.random.standard_normal((E, D)) * s)
    x_edge_c = bf(np.random.standard_normal((E, H)) * t)
    ori = bf(np.random.standard_normal((E, D)) * s)
    W1_words, W1_scales = pack_weight(np.random.standard_normal((D, H)) * 1.0 / np.sqrt(D) / s[:, None], "e4m3")
    b1 = bf(np.random.standard_normal(H) * 0.3)
    W2_words, W2_scales = pack_weight(np.random.standard_normal((H, D)) * 1.5 / np.sqrt(H) / t[:, None], "e4m3")
    b2 = bf(np.random.standard_normal(D) * 0.3)
    return {
        "node_embed": node_embed,
        "x_edge_c": x_edge_c,
        "ori": ori,
        "W1_words": W1_words,
        "W1_scales": W1_scales,
        "b1": b1,
        "W2_words": W2_words,
        "W2_scales": W2_scales,
        "b2": b2,
        "edge_num": E,
    }


def reference(node_embed, x_edge_c, ori, W1_words, W1_scales, b1, W2_words, W2_scales, b2, edge_num):
    x = np.concatenate([f64(node_embed), f64(ori)], axis=0)
    h = silu((mxq(x, 1, "e4m3") @ unpack_weight(W1_words, W1_scales, "e4m3")) + f64(b1))
    h = (h.reshape(2, edge_num, H) * f64(x_edge_c).reshape(1, edge_num, H)).reshape(-1, H)
    y = silu((mxq(h, 1, "e4m3") @ unpack_weight(W2_words, W2_scales, "e4m3")) + f64(b2))
    y = y.reshape(2 * edge_num, -1, C)
    return y[:edge_num] + y[edge_num:]

@@ -1,0 +1,250 @@
+from contextlib import ExitStack
+
+import concourse.mybir as mybir
+from concourse.masks import make_identity
+
+F32 = mybir.dt.float32
+BF16 = mybir.dt.bfloat16
+I32 = mybir.dt.int32
+U32 = mybir.dt.uint32
+U8 = mybir.dt.uint8
+FP8X4 = mybir.dt.float8_e4m3fn_x4
+ACT = mybir.ActivationFunctionType
+ALU = mybir.AluOpType
+
+P = 128
+E = 128
+D = 2048
+H = 4096
+G1 = D // 512
+G2 = H // 512
+NC = 512
+
+FLOPS = 2 * (2 * E) * D * H * 2
+
+
+def tile_node_interaction_w_kernel(
+    tc, node_embed, x_edge_c, ori, W1_words, W1_scales, b1, W2_words, W2_scales, b2, edge_num, out
+):
+    nc = tc.nc
+    assert edge_num == E
+    with ExitStack() as ctx:
+        keep = ctx.enter_context(tc.tile_pool(name="keep", bufs=1))
+        work = ctx.enter_context(tc.tile_pool(name="work", bufs=2))
+        psum = ctx.enter_context(tc.psum_pool(name="psum", bufs=4))
+
+        w1_sb = keep.tile([P, G1, H], U32, align_bytes=64)
+        w2_sb = keep.tile([P, G2, D], U32, align_bytes=64)
+        planes1 = keep.tile([P, H], U8, align_bytes=64)
+        planes2 = keep.tile([P, 2, D], U8, align_bytes=64)
+        x_sb = keep.tile([P, 2, D], BF16, align_bytes=64)
+        xe_sb = keep.tile([P, H], BF16, align_bytes=64)
+        xg = keep.tile([P, G1, 2, E, 4], BF16, align_bytes=64)
+        xq = keep.tile([P, G1, 2 * E], U32, align_bytes=64)
+        xs = keep.tile([P, G1, 2 * E], U8, align_bytes=64)
+        gT = keep.tile([P, G2, E, 4], BF16, align_bytes=64)
+        hq = keep.tile([P, G2, 2 * E], U32, align_bytes=64)
+        hs = keep.tile([P, G2, 2 * E], U8, align_bytes=64)
+        b2z = keep.tile([P, D], BF16, align_bytes=64)
+        b2bc = keep.tile([P, D], F32)
+        b1raw = keep.tile([P, G2, 4], BF16)
+        b1c = keep.tile([P, G2 * 4], F32)
+        ident = keep.tile([P, P], F32)
+        ones = keep.tile([P, P], BF16)
+
+        nc.vector.memset(planes1[:].bitcast(I32), 0)
+        nc.vector.memset(b2z[:].bitcast(I32), 0)
+        nc.vector.memset(planes2[:].rearrange("p a n -> p (a n)").bitcast(I32), 0)
+        make_identity(nc, ident[:])
+        nc.gpsimd.memset(ones[:], 1.0)
+
+        w1v = W1_words.rearrange("g p n t -> g p (n t)").bitcast(I32)
+        w2v = W2_words.rearrange("g p n t -> g p (n t)").bitcast(I32)
+        s1v = W1_scales.bitcast(I32)
+        s2v = W2_scales.bitcast(I32)
+
+        def load_w1(n0, n1):
+            nc.sync.dma_start(
+                out=w1_sb[:, :, n0:n1].bitcast(I32),
+                in_=w1v[:, :, n0:n1].rearrange("g p n -> p g n"),
+            )
+
+        def load_w2(n0, n1):
+            nc.sync.dma_start(
+                out=w2_sb[:, :, n0:n1].bitcast(I32),
+                in_=w2v[:, :, n0:n1].rearrange("g p n -> p g n"),
+            )
+
+        nc.sync.dma_start(out=x_sb[:, 0, :], in_=node_embed)
+        nc.sync.dma_start(out=x_sb[:, 1, :], in_=ori)
+        for q in range(4):
+            nc.sync.dma_start(
+                out=planes1[32 * q : 32 * q + 16, :].bitcast(I32),
+                in_=s1v[:, 4 * q : 4 * q + 4, :],
+            )
+        load_w1(0, 512)
+        nc.sync.dma_start(out=b2z[0:1, :], in_=b2.rearrange("(o n) -> o n", o=1))
+        nc.sync.dma_start(out=b1raw[:], in_=b1.rearrange("(g p t) -> p g t", g=G2, p=P, t=4))
+        load_w1(512, 1024)
+        nc.sync.dma_start(out=xe_sb[:, 0:2048], in_=x_edge_c[:, 0:2048])
+        load_w1(1024, 2048)
+        nc.sync.dma_start(out=xe_sb[:, 2048:4096], in_=x_edge_c[:, 2048:4096])
+        load_w1(2048, 3072)
+        load_w1(3072, 4096)
+        for a in range(2):
+            for q in range(4):
+                nc.sync.dma_start(
+                    out=planes2[32 * q : 32 * q + 16, a, :].bitcast(I32),
+                    in_=s2v[4 * a : 4 * a + 4, 4 * q : 4 * q + 4, :],
+                )
+        for j in range(4):
+            load_w2(512 * j, 512 * j + 512)
+
+        for g in range(G1):
+            xT = psum.tile([P, 2, 2, E], F32, tag="T")
+            for h in range(2):
+                xw = x_sb[:, h, :].bitcast(F32)
+                for u in range(2):
+                    nc.tensor.transpose(xT[:, h, u, :], xw[:, 256 * g + u : 256 * (g + 1) : 2], ident[:])
+            dst = xg[:, g].bitcast(F32)
+            src = xT[:].rearrange("p h u r -> p h r u")
+            if g % 2 == 0:
+                nc.vector.tensor_copy(out=dst, in_=src)
+            else:
+                nc.scalar.copy(out=dst, in_=src)
+        for g in range(G1):
+            nc.vector.quantize_mx(
+                out=xq[:, g, :].bitcast(FP8X4),
+                scales=xs[:, g, :],
+                in_=xg[:, g].rearrange("p h r t -> p (h r t)"),
+            )
+
+        for j in range(4):
+            bps = psum.tile([P, NC], F32, tag="T")
+            nc.tensor.matmul(out=bps[:], lhsT=ones[:], rhs=b2z[:, NC * j : NC * (j + 1)], start=True, stop=True)
+            nc.scalar.copy(out=b2bc[:, NC * j : NC * (j + 1)], in_=bps[:])
+        nc.vector.tensor_copy(out=b1c[:], in_=b1raw[:].rearrange("p g t -> p (g t)"))
+
+        xew = xe_sb[:].bitcast(F32)
+        state = {}
+
+        def gate(c):
+            gps = psum.tile([P, 2, 2, E], F32, tag="T")
+            for gg in range(2):
+                for u in range(2):
+                    nc.tensor.transpose(
+                        gps[:, gg, u, :], xew[:, 256 * (c + gg) + u : 256 * (c + gg + 1) : 2], ident[:]
+                    )
+            nc.scalar.copy(out=gT[:, c : c + 2].bitcast(F32), in_=gps[:].rearrange("p g u r -> p g r u"))
+
+        def passes1(c):
+            accs = []
+            for h in range(2):
+                acc = psum.tile([P, NC], F32, tag="acc", name="acc1_%d_%d" % (c, h))
+                for g in range(G1):
+                    nc.tensor.matmul_mx(
+                        out=acc[:],
+                        lhsT=xq[:, g, E * h : E * (h + 1)].bitcast(FP8X4),
+                        lhsT_scale=xs[:, g, E * h : E * (h + 1)],
+                        rhs=w1_sb[:, g, NC * c : NC * (c + 1)].bitcast(FP8X4),
+                        rhs_scale=planes1[4 * g : P, NC * c : NC * (c + 1)],
+                        start=(g == 0),
+                        stop=(g == G1 - 1),
+                    )
+                accs.append(acc)
+            state[("acc", c)] = accs
+
+        def sort_out(c):
+            accs = state[("acc", c)]
+            srt = work.tile([P, 2, 4, E], F32, tag="st1", name="srt_%d" % c)
+            nc.vector.tensor_copy(out=srt[:, 0], in_=accs[0][:].rearrange("p (q t) -> p t q", t=4))
+            nc.scalar.copy(out=srt[:, 1], in_=accs[1][:].rearrange("p (q t) -> p t q", t=4))
+            state[("srt", c)] = srt
+
+        def flip(c):
+            srt = state[("srt", c)]
+            tps = []
+            for tt in range(2):
+                tp = psum.tile([P, 2, 2, E], F32, tag="T", name="tp_%d_%d" % (c, tt))
+                for t2 in range(2):
+                    for h in range(2):
+                        nc.tensor.transpose(tp[:, t2, h, :], srt[:, h, 2 * tt + t2, :], ident[:])
+                tps.append(tp)
+            state[("tp", c)] = tps
+
+        def finish1(c):
+            tps = state[("tp", c)]
+            act = work.tile([P, 4, 2, E], F32, tag="st2", name="act_%d" % c)
+            for t in range(4):
+                nc.scalar.activation(
+                    out=act[:, t],
+                    in_=tps[t // 2][:, t % 2],
+                    func=ACT.Silu,
+                    bias=b1c[:, 4 * c + t : 4 * c + t + 1],
+                )
+            hg = work.tile([P, 2, E, 4], BF16, tag="hg", name="hg_%d" % c, align_bytes=64)
+            nc.vector.tensor_tensor(
+                out=hg[:],
+                in0=act[:].rearrange("p t h r -> p h r t"),
+                in1=gT[:, c].unsqueeze(1).to_broadcast([P, 2, E, 4]),
+                op=ALU.mult,
+            )
+            nc.vector.quantize_mx(
+                out=hq[:, c, :].bitcast(FP8X4),
+                scales=hs[:, c, :],
+                in_=hg[:].rearrange("p h r t -> p (h r t)"),
+            )
+
+        def open2(j):
+            state[("acc2", j)] = [
+                psum.tile([P, NC], F32, tag="acc", name="acc2_%d_%d" % (j, h)) for h in range(2)
+            ]
+
+        def passes2(j, g_list):
+            accs = state[("acc2", j)]
+            for g in g_list:
+                for h in range(2):
+                    nc.tensor.matmul_mx(
+                        out=accs[h][:],
+                        lhsT=hq[:, g, E * h : E * (h + 1)].bitcast(FP8X4),
+                        lhsT_scale=hs[:, g, E * h : E * (h + 1)],
+                        rhs=w2_sb[:, g, NC * j : NC * (j + 1)].bitcast(FP8X4),
+                        rhs_scale=planes2[4 * (g % 4) : P, g // 4, NC * j : NC * (j + 1)],
+                        start=(g == 0),
+                        stop=(g == G2 - 1),
+                    )
+
+        out2d = out.rearrange("e a c -> e (a c)")
+
+        def finish2(j):
+            accs = state[("acc2", j)]
+            cols = slice(NC * j, NC * (j + 1))
+            pre = work.tile([P, 2, NC], F32, tag="st1", name="pre_%d" % j)
+            post = work.tile([P, 2, NC], F32, tag="st2", name="post_%d" % j)
+            for h in range(2):
+                nc.vector.tensor_tensor(out=pre[:, h, :], in0=accs[h][:], in1=b2bc[:, cols], op=ALU.add)
+                nc.scalar.activation(out=post[:, h, :], in_=pre[:, h, :], func=ACT.Silu)
+            res = work.tile([P, NC], F32, tag="res", name="res_%d" % j)
+            nc.vector.tensor_tensor(out=res[:], in0=post[:, 0, :], in1=post[:, 1, :], op=ALU.add)
+            nc.sync.dma_start(out=out2d[:, cols], in_=res[:])
+
+        passes1(0)
+        sort_out(0)
+        gate(0)
+        for c in range(1, G2):
+            passes1(c)
+            flip(c - 1)
+            if c % 2 == 0:
+                gate(c)
+            sort_out(c)
+            finish1(c - 1)
+        open2(0)
+        passes2(0, range(0, 6))
+        flip(G2 - 1)
+        finish1(G2 - 1)
+        passes2(0, range(6, G2))
+        for j in range(1, 4):
+            open2(j)
+            passes2(j, range(G2))
+            finish2(j - 1)
+        finish2(3)

@@ -29,9 +29,10 @@ def tile_node_interaction_w_kernel(
     nc = tc.nc
     assert edge_num == E
     with ExitStack() as ctx:
+        ctx.enter_context(tc.manual_schedule())
         keep = ctx.enter_context(tc.tile_pool(name="keep", bufs=1))
         work = ctx.enter_context(tc.tile_pool(name="work", bufs=2))
-        psum = ctx.enter_context(tc.psum_pool(name="psum", bufs=4))
+        psum = ctx.enter_context(tc.psum_pool(name="psum", bufs=2))
 
         w1_sb = keep.tile([P, G1, H], U32, align_bytes=64)
         w2_sb = keep.tile([P, G2, D], U32, align_bytes=64)
@@ -42,72 +43,86 @@ def tile_node_interaction_w_kernel(
         xg = keep.tile([P, G1, 2, E, 4], BF16, align_bytes=64)
         xq = keep.tile([P, G1, 2 * E], U32, align_bytes=64)
         xs = keep.tile([P, G1, 2 * E], U8, align_bytes=64)
-        gT = keep.tile([P, G2, E, 4], BF16, align_bytes=64)
         hq = keep.tile([P, G2, 2 * E], U32, align_bytes=64)
         hs = keep.tile([P, G2, 2 * E], U8, align_bytes=64)
+        b1z = keep.tile([P, H], BF16, align_bytes=64)
         b2z = keep.tile([P, D], BF16, align_bytes=64)
-        b2bc = keep.tile([P, D], F32)
-        b1raw = keep.tile([P, G2, 4], BF16)
-        b1c = keep.tile([P, G2 * 4], F32)
-        ident = keep.tile([P, P], F32)
+        b1bc = keep.tile([P, G2, 4, E], BF16)
+        b2bc = keep.tile([P, D], BF16)
+        identf = keep.tile([P, P], F32)
+        identb = keep.tile([P, P], BF16)
         ones = keep.tile([P, P], BF16)
 
         nc.vector.memset(planes1[:].bitcast(I32), 0)
+        nc.vector.memset(b1z[:].bitcast(I32), 0)
         nc.vector.memset(b2z[:].bitcast(I32), 0)
         nc.vector.memset(planes2[:].rearrange("p a n -> p (a n)").bitcast(I32), 0)
-        make_identity(nc, ident[:])
+        make_identity(nc, identf[:])
         nc.gpsimd.memset(ones[:], 1.0)
+        make_identity(nc, identb[:])
 
         w1v = W1_words.rearrange("g p n t -> g p (n t)").bitcast(I32)
         w2v = W2_words.rearrange("g p n t -> g p (n t)").bitcast(I32)
         s1v = W1_scales.bitcast(I32)
         s2v = W2_scales.bitcast(I32)
 
-        def load_w1(n0, n1):
+        def load_w1(g0, g1, n0, n1):
             nc.sync.dma_start(
-                out=w1_sb[:, :, n0:n1].bitcast(I32),
-                in_=w1v[:, :, n0:n1].rearrange("g p n -> p g n"),
+                out=w1_sb[:, g0:g1, n0:n1].bitcast(I32),
+                in_=w1v[g0:g1, :, n0:n1].rearrange("g p n -> p g n"),
             )
 
-        def load_w2(n0, n1):
+        def load_w2(g0, g1, n0, n1):
             nc.sync.dma_start(
-                out=w2_sb[:, :, n0:n1].bitcast(I32),
-                in_=w2v[:, :, n0:n1].rearrange("g p n -> p g n"),
+                out=w2_sb[:, g0:g1, n0:n1].bitcast(I32),
+                in_=w2v[g0:g1, :, n0:n1].rearrange("g p n -> p g n"),
             )
+
+        def load_s1(n0, n1):
+            for q in range(4):
+                nc.sync.dma_start(
+                    out=planes1[32 * q : 32 * q + 16, n0:n1].bitcast(I32),
+                    in_=s1v[:, 4 * q : 4 * q + 4, n0 // 4 : n1 // 4],
+                )
 
         nc.sync.dma_start(out=x_sb[:, 0, :], in_=node_embed)
         nc.sync.dma_start(out=x_sb[:, 1, :], in_=ori)
-        for q in range(4):
-            nc.sync.dma_start(
-                out=planes1[32 * q : 32 * q + 16, :].bitcast(I32),
-                in_=s1v[:, 4 * q : 4 * q + 4, :],
-            )
-        load_w1(0, 512)
-        nc.sync.dma_start(out=b2z[0:1, :], in_=b2.rearrange("(o n) -> o n", o=1))
-        nc.sync.dma_start(out=b1raw[:], in_=b1.rearrange("(g p t) -> p g t", g=G2, p=P, t=4))
-        load_w1(512, 1024)
-        nc.sync.dma_start(out=xe_sb[:, 0:2048], in_=x_edge_c[:, 0:2048])
-        load_w1(1024, 2048)
-        nc.sync.dma_start(out=xe_sb[:, 2048:4096], in_=x_edge_c[:, 2048:4096])
-        load_w1(2048, 3072)
-        load_w1(3072, 4096)
+        nc.scalar.dma_start(out=b1z[0:1, :], in_=b1.rearrange("(o n) -> o n", o=1))
+        nc.scalar.dma_start(out=b2z[0:1, :], in_=b2.rearrange("(o n) -> o n", o=1))
+        load_s1(0, 1024)
+        load_w1(0, 2, 0, 512)
+        load_w1(2, 4, 0, 512)
+        nc.sync.dma_start(out=xe_sb[:, 0:1024], in_=x_edge_c[:, 0:1024])
+        load_w1(0, 4, 512, 1024)
+        load_s1(1024, 4096)
+        load_w1(0, 4, 1024, 2048)
+        nc.sync.dma_start(out=xe_sb[:, 1024:4096], in_=x_edge_c[:, 1024:4096])
+        load_w1(0, 4, 2048, 3072)
+        load_w1(0, 4, 3072, 4096)
         for a in range(2):
             for q in range(4):
                 nc.sync.dma_start(
                     out=planes2[32 * q : 32 * q + 16, a, :].bitcast(I32),
                     in_=s2v[4 * a : 4 * a + 4, 4 * q : 4 * q + 4, :],
                 )
-        for j in range(4):
-            load_w2(512 * j, 512 * j + 512)
+        for gp in range(4):
+            load_w2(2 * gp, 2 * gp + 2, 0, 1024)
+        load_w2(0, 4, 1024, 1536)
+        load_w2(4, 8, 1024, 1536)
+        load_w2(0, 8, 1536, 1792)
+        load_w2(0, 8, 1792, 2048)
 
+        xts = []
         for g in range(G1):
-            xT = psum.tile([P, 2, 2, E], F32, tag="T")
+            xT = psum.tile([P, 2, 2, E], F32, tag="acc", bufs=4, name="xT_%d" % g)
             for h in range(2):
                 xw = x_sb[:, h, :].bitcast(F32)
                 for u in range(2):
-                    nc.tensor.transpose(xT[:, h, u, :], xw[:, 256 * g + u : 256 * (g + 1) : 2], ident[:])
+                    nc.tensor.transpose(xT[:, h, u, :], xw[:, 256 * g + u : 256 * (g + 1) : 2], identf[:])
+            xts.append(xT)
+        for g in (0, 2, 1, 3):
             dst = xg[:, g].bitcast(F32)
-            src = xT[:].rearrange("p h u r -> p h r u")
+            src = xts[g][:].rearrange("p h u r -> p h r u")
             if g % 2 == 0:
                 nc.vector.tensor_copy(out=dst, in_=src)
             else:
@@ -119,132 +134,177 @@ def tile_node_interaction_w_kernel(
                 in_=xg[:, g].rearrange("p h r t -> p (h r t)"),
             )
 
-        for j in range(4):
-            bps = psum.tile([P, NC], F32, tag="T")
-            nc.tensor.matmul(out=bps[:], lhsT=ones[:], rhs=b2z[:, NC * j : NC * (j + 1)], start=True, stop=True)
-            nc.scalar.copy(out=b2bc[:, NC * j : NC * (j + 1)], in_=bps[:])
-        nc.vector.tensor_copy(out=b1c[:], in_=b1raw[:].rearrange("p g t -> p (g t)"))
+        bc_count = [0]
 
-        xew = xe_sb[:].bitcast(F32)
+        def spread(which, idx):
+            k = bc_count[0]
+            bc_count[0] = k + 1
+            bps = psum.tile([P, NC], F32, tag=("mi" if k % 4 < 2 else "tp"), name="bps_%d" % k)
+            src_z = b1z if which == 1 else b2z
+            nc.tensor.matmul(out=bps[:], lhsT=ones[:], rhs=src_z[:, NC * idx : NC * (idx + 1)], start=True, stop=True)
+            if which == 1:
+                dst = b1bc[:, idx]
+                src = bps[:].rearrange("p (q t) -> p t q", t=4)
+            else:
+                dst = b2bc[:, NC * idx : NC * (idx + 1)]
+                src = bps[:]
+            if k % 2 == 0:
+                nc.scalar.copy(out=dst, in_=src)
+            else:
+                nc.vector.tensor_copy(out=dst, in_=src)
+
         state = {}
 
-        def gate(c):
-            gps = psum.tile([P, 2, 2, E], F32, tag="T")
-            for gg in range(2):
-                for u in range(2):
-                    nc.tensor.transpose(
-                        gps[:, gg, u, :], xew[:, 256 * (c + gg) + u : 256 * (c + gg + 1) : 2], ident[:]
-                    )
-            nc.scalar.copy(out=gT[:, c : c + 2].bitcast(F32), in_=gps[:].rearrange("p g u r -> p g r u"))
+        def mx1(acc, c, h, g):
+            nc.tensor.matmul_mx(
+                out=acc[:],
+                lhsT=xq[:, g, E * h : E * (h + 1)].bitcast(FP8X4),
+                lhsT_scale=xs[:, g, E * h : E * (h + 1)],
+                rhs=w1_sb[:, g, NC * c : NC * (c + 1)].bitcast(FP8X4),
+                rhs_scale=planes1[4 * g : P, NC * c : NC * (c + 1)],
+                start=(g == 0),
+                stop=(g == G1 - 1),
+            )
 
         def passes1(c):
-            accs = []
-            for h in range(2):
-                acc = psum.tile([P, NC], F32, tag="acc", name="acc1_%d_%d" % (c, h))
-                for g in range(G1):
-                    nc.tensor.matmul_mx(
-                        out=acc[:],
-                        lhsT=xq[:, g, E * h : E * (h + 1)].bitcast(FP8X4),
-                        lhsT_scale=xs[:, g, E * h : E * (h + 1)],
-                        rhs=w1_sb[:, g, NC * c : NC * (c + 1)].bitcast(FP8X4),
-                        rhs_scale=planes1[4 * g : P, NC * c : NC * (c + 1)],
-                        start=(g == 0),
-                        stop=(g == G1 - 1),
-                    )
-                accs.append(acc)
+            accs = [psum.tile([P, NC], F32, tag="acc", bufs=4, name="acc1_%d_%d" % (c, h)) for h in range(2)]
+            if c == 0:
+                order = [(0, 0), (0, 1), (1, 0), (1, 1), (0, 2), (0, 3), (1, 2), (1, 3)]
+            else:
+                order = [(h, g) for h in range(2) for g in range(G1)]
+            for h, g in order:
+                mx1(accs[h], c, h, g)
             state[("acc", c)] = accs
+            state[("pre", c)] = work.tile([P, 2, 4, E], F32, tag="pre", name="pre_%d" % c)
+            state[("hsrt", c)] = work.tile([P, 2, 4, E], BF16, tag="hsrt", bufs=3, name="hsrt_%d" % c)
 
-        def sort_out(c):
-            accs = state[("acc", c)]
-            srt = work.tile([P, 2, 4, E], F32, tag="st1", name="srt_%d" % c)
-            nc.vector.tensor_copy(out=srt[:, 0], in_=accs[0][:].rearrange("p (q t) -> p t q", t=4))
-            nc.scalar.copy(out=srt[:, 1], in_=accs[1][:].rearrange("p (q t) -> p t q", t=4))
-            state[("srt", c)] = srt
-
-        def flip(c):
-            srt = state[("srt", c)]
-            tps = []
-            for tt in range(2):
-                tp = psum.tile([P, 2, 2, E], F32, tag="T", name="tp_%d_%d" % (c, tt))
-                for t2 in range(2):
-                    for h in range(2):
-                        nc.tensor.transpose(tp[:, t2, h, :], srt[:, h, 2 * tt + t2, :], ident[:])
-                tps.append(tp)
-            state[("tp", c)] = tps
-
-        def finish1(c):
-            tps = state[("tp", c)]
-            act = work.tile([P, 4, 2, E], F32, tag="st2", name="act_%d" % c)
-            for t in range(4):
-                nc.scalar.activation(
-                    out=act[:, t],
-                    in_=tps[t // 2][:, t % 2],
-                    func=ACT.Silu,
-                    bias=b1c[:, 4 * c + t : 4 * c + t + 1],
-                )
-            hg = work.tile([P, 2, E, 4], BF16, tag="hg", name="hg_%d" % c, align_bytes=64)
+        def add1(c, h):
             nc.vector.tensor_tensor(
-                out=hg[:],
-                in0=act[:].rearrange("p t h r -> p h r t"),
-                in1=gT[:, c].unsqueeze(1).to_broadcast([P, 2, E, 4]),
+                out=state[("pre", c)][:, h],
+                in0=state[("acc", c)][h][:].rearrange("p (q t) -> p t q", t=4),
+                in1=b1bc[:, c],
+                op=ALU.add,
+            )
+
+        def silu1(c, h):
+            pre = state[("pre", c)]
+            nc.scalar.activation(out=pre[:, h], in_=pre[:, h], func=ACT.Silu)
+
+        def mult1(c, h):
+            eng = nc.vector if h == 0 else nc.gpsimd
+            eng.tensor_tensor(
+                out=state[("hsrt", c)][:, h],
+                in0=state[("pre", c)][:, h],
+                in1=xe_sb[:, NC * c : NC * (c + 1)].rearrange("p (q t) -> p t q", t=4),
                 op=ALU.mult,
             )
+
+        def flip(c):
+            hsrt = state[("hsrt", c)]
+            tp = psum.tile([P, 2, 4, E], BF16, tag="tp", name="tp_%d" % c)
+            for h in range(2):
+                for t in range(4):
+                    nc.tensor.transpose(tp[:, h, t, :], hsrt[:, h, t, :], identb[:])
+            state[("tp", c)] = tp
+
+        def copyout(c):
+            hg = work.tile([P, 2, E, 4], BF16, tag="hg", name="hg_%d" % c, align_bytes=64)
+            nc.scalar.copy(out=hg[:], in_=state[("tp", c)][:].rearrange("p h t r -> p h r t"))
+            state[("hg", c)] = hg
+
+        def quant(c):
             nc.vector.quantize_mx(
                 out=hq[:, c, :].bitcast(FP8X4),
                 scales=hs[:, c, :],
-                in_=hg[:].rearrange("p h r t -> p (h r t)"),
+                in_=state[("hg", c)][:].rearrange("p h r t -> p (h r t)"),
             )
 
-        def open2(j):
-            state[("acc2", j)] = [
-                psum.tile([P, NC], F32, tag="acc", name="acc2_%d_%d" % (j, h)) for h in range(2)
-            ]
-
-        def passes2(j, g_list):
-            accs = state[("acc2", j)]
-            for g in g_list:
-                for h in range(2):
-                    nc.tensor.matmul_mx(
-                        out=accs[h][:],
-                        lhsT=hq[:, g, E * h : E * (h + 1)].bitcast(FP8X4),
-                        lhsT_scale=hs[:, g, E * h : E * (h + 1)],
-                        rhs=w2_sb[:, g, NC * j : NC * (j + 1)].bitcast(FP8X4),
-                        rhs_scale=planes2[4 * (g % 4) : P, g // 4, NC * j : NC * (j + 1)],
-                        start=(g == 0),
-                        stop=(g == G2 - 1),
-                    )
+        def mx2(acc, h, g, n0, n1):
+            nc.tensor.matmul_mx(
+                out=acc[:],
+                lhsT=hq[:, g, E * h : E * (h + 1)].bitcast(FP8X4),
+                lhsT_scale=hs[:, g, E * h : E * (h + 1)],
+                rhs=w2_sb[:, g, n0:n1].bitcast(FP8X4),
+                rhs_scale=planes2[4 * (g % 4) : P, g // 4, n0:n1],
+                start=(g == 0),
+                stop=(g == G2 - 1),
+            )
 
         out2d = out.rearrange("e a c -> e (a c)")
 
-        def finish2(j):
-            accs = state[("acc2", j)]
-            cols = slice(NC * j, NC * (j + 1))
-            pre = work.tile([P, 2, NC], F32, tag="st1", name="pre_%d" % j)
-            post = work.tile([P, 2, NC], F32, tag="st2", name="post_%d" % j)
+        def finish2(accs, n0, n1):
+            w = n1 - n0
+            pre = work.tile([P, 2, NC], F32, tag="pre", name="pre2_%d" % n0)
             for h in range(2):
-                nc.vector.tensor_tensor(out=pre[:, h, :], in0=accs[h][:], in1=b2bc[:, cols], op=ALU.add)
-                nc.scalar.activation(out=post[:, h, :], in_=pre[:, h, :], func=ACT.Silu)
-            res = work.tile([P, NC], F32, tag="res", name="res_%d" % j)
-            nc.vector.tensor_tensor(out=res[:], in0=post[:, 0, :], in1=post[:, 1, :], op=ALU.add)
-            nc.sync.dma_start(out=out2d[:, cols], in_=res[:])
+                nc.vector.tensor_tensor(out=pre[:, h, 0:w], in0=accs[h][:], in1=b2bc[:, n0:n1], op=ALU.add)
+                nc.scalar.activation(out=pre[:, h, 0:w], in_=pre[:, h, 0:w], func=ACT.Silu)
+            res = work.tile([P, NC], F32, tag="res", name="res_%d" % n0)
+            nc.vector.tensor_tensor(out=res[:, 0:w], in0=pre[:, 0, 0:w], in1=pre[:, 1, 0:w], op=ALU.add)
+            nc.sync.dma_start(out=out2d[:, n0:n1], in_=res[:, 0:w])
 
-        passes1(0)
-        sort_out(0)
-        gate(0)
-        for c in range(1, G2):
-            passes1(c)
-            flip(c - 1)
-            if c % 2 == 0:
-                gate(c)
-            sort_out(c)
-            finish1(c - 1)
-        open2(0)
-        passes2(0, range(0, 6))
-        flip(G2 - 1)
-        finish1(G2 - 1)
-        passes2(0, range(6, G2))
-        for j in range(1, 4):
-            open2(j)
-            passes2(j, range(G2))
-            finish2(j - 1)
-        finish2(3)
+        for idx in range(4):
+            spread(1, idx)
+        for i in range(G2):
+            passes1(i)
+            if i >= 2:
+                flip(i - 2)
+            add1(i, 0)
+            if i >= 3:
+                quant(i - 3)
+            add1(i, 1)
+            silu1(i, 0)
+            silu1(i, 1)
+            mult1(i, 0)
+            mult1(i, 1)
+            if i >= 2:
+                copyout(i - 2)
+            if i == 0:
+                for idx in range(4, 8):
+                    spread(1, idx)
+            if i == 1:
+                for idx in range(4):
+                    spread(2, idx)
+
+        blk0 = [
+            (psum.tile([P, NC], F32, tag="acc", bufs=4, name="acc2_%d_%d" % (j, h)), h, NC * j)
+            for j in range(2)
+            for h in range(2)
+        ]
+
+        def blk0_passes(g_list):
+            for acc, h, n0 in blk0:
+                for g in g_list:
+                    mx2(acc, h, g, n0, n0 + NC)
+
+        blk0_passes((0, 1))
+        flip(6)
+        flip(7)
+        quant(5)
+        copyout(6)
+        quant(6)
+        copyout(7)
+        quant(7)
+        blk0_passes((2, 3))
+        blk0_passes((4, 5))
+        blk0_passes((6, 7))
+
+        blk1 = [psum.tile([P, NC], F32, tag="mi", name="acc2b_%d" % h) for h in range(2)]
+        for g_list in ((0, 1, 2, 3), (4, 5, 6, 7)):
+            for h in range(2):
+                for g in g_list:
+                    mx2(blk1[h], h, g, 1024, 1536)
+        finish2([blk0[0][0], blk0[1][0]], 0, 512)
+        finish2([blk0[2][0], blk0[3][0]], 512, 1024)
+
+        blk2 = [psum.tile([P, 256], F32, tag="tp", name="acc2c_%d" % h) for h in range(2)]
+        for h in range(2):
+            for g in range(G2):
+                mx2(blk2[h], h, g, 1536, 1792)
+        finish2(blk1, 1024, 1536)
+
+        blk3 = [psum.tile([P, 256], F32, tag="acc", bufs=4, name="acc2d_%d" % h) for h in range(2)]
+        for h in range(2):
+            for g in range(G2):
+                mx2(blk3[h], h, g, 1792, 2048)
+        finish2(blk2, 1536, 1792)
+        finish2(blk3, 1792, 2048)

@@ -53,18 +53,16 @@ def tile_node_interaction_w_kernel(
         identb = keep.tile([P, P], BF16)
         ones = keep.tile([P, P], BF16)
 
-        nc.vector.memset(planes1[:].bitcast(I32), 0)
         nc.vector.memset(b1z[:].bitcast(I32), 0)
-        nc.vector.memset(b2z[:].bitcast(I32), 0)
+        nc.vector.memset(planes1[:].bitcast(I32), 0)
         nc.vector.memset(planes2[:].rearrange("p a n -> p (a n)").bitcast(I32), 0)
-        make_identity(nc, identf[:])
+        nc.vector.memset(b2z[:].bitcast(I32), 0)
         nc.gpsimd.memset(ones[:], 1.0)
-        make_identity(nc, identb[:])
+        make_identity(nc, identf[:])
 
         w1v = W1_words.rearrange("g p n t -> g p (n t)").bitcast(I32)
         w2v = W2_words.rearrange("g p n t -> g p (n t)").bitcast(I32)
         s1v = W1_scales.bitcast(I32)
-        s2v = W2_scales.bitcast(I32)
 
         def load_w1(g0, g1, n0, n1):
             nc.sync.dma_start(
@@ -85,32 +83,38 @@ def tile_node_interaction_w_kernel(
                     in_=s1v[:, 4 * q : 4 * q + 4, n0 // 4 : n1 // 4],
                 )
 
+        nc.scalar.dma_start(out=b1z[0:1, :], in_=b1.rearrange("(o n) -> o n", o=1))
         nc.sync.dma_start(out=x_sb[:, 0, :], in_=node_embed)
         nc.sync.dma_start(out=x_sb[:, 1, :], in_=ori)
-        nc.scalar.dma_start(out=b1z[0:1, :], in_=b1.rearrange("(o n) -> o n", o=1))
-        nc.scalar.dma_start(out=b2z[0:1, :], in_=b2.rearrange("(o n) -> o n", o=1))
         load_s1(0, 1024)
         load_w1(0, 2, 0, 512)
         load_w1(2, 4, 0, 512)
-        nc.sync.dma_start(out=xe_sb[:, 0:1024], in_=x_edge_c[:, 0:1024])
         load_w1(0, 4, 512, 1024)
+        nc.sync.dma_start(out=xe_sb[:, 0:1024], in_=x_edge_c[:, 0:1024])
+        nc.sync.dma_start(out=b2z[0:1, :], in_=b2.rearrange("(o n) -> o n", o=1))
         load_s1(1024, 4096)
-        load_w1(0, 4, 1024, 2048)
+        load_w1(0, 2, 1024, 2048)
+        load_w1(2, 4, 1024, 2048)
         nc.sync.dma_start(out=xe_sb[:, 1024:4096], in_=x_edge_c[:, 1024:4096])
-        load_w1(0, 4, 2048, 3072)
-        load_w1(0, 4, 3072, 4096)
+        load_w1(0, 2, 2048, 3072)
+        load_w1(2, 4, 2048, 3072)
+        load_w1(0, 2, 3072, 4096)
+        load_w1(2, 4, 3072, 4096)
+        s2f = W2_scales.bitcast(F32)
         for a in range(2):
             for q in range(4):
-                nc.sync.dma_start(
-                    out=planes2[32 * q : 32 * q + 16, a, :].bitcast(I32),
-                    in_=s2v[4 * a : 4 * a + 4, 4 * q : 4 * q + 4, :],
+                nc.gpsimd.dma_start(
+                    out=planes2[32 * q : 32 * q + 16, a, :].bitcast(F32),
+                    in_=s2f[4 * a : 4 * a + 4, 4 * q : 4 * q + 4, :],
                 )
+        make_identity(nc, identb[:])
         for gp in range(4):
             load_w2(2 * gp, 2 * gp + 2, 0, 1024)
         load_w2(0, 4, 1024, 1536)
         load_w2(4, 8, 1024, 1536)
         load_w2(0, 8, 1536, 1792)
-        load_w2(0, 8, 1792, 2048)
+        load_w2(0, 4, 1792, 2048)
+        load_w2(4, 8, 1792, 2048)
 
         xts = []
         for g in range(G1):
@@ -166,17 +170,29 @@ def tile_node_interaction_w_kernel(
                 stop=(g == G1 - 1),
             )
 
-        def passes1(c):
-            accs = [psum.tile([P, NC], F32, tag="acc", bufs=4, name="acc1_%d_%d" % (c, h)) for h in range(2)]
-            if c == 0:
-                order = [(0, 0), (0, 1), (1, 0), (1, 1), (0, 2), (0, 3), (1, 2), (1, 3)]
-            else:
-                order = [(h, g) for h in range(2) for g in range(G1)]
-            for h, g in order:
-                mx1(accs[h], c, h, g)
-            state[("acc", c)] = accs
-            state[("pre", c)] = work.tile([P, 2, 4, E], F32, tag="pre", name="pre_%d" % c)
-            state[("hsrt", c)] = work.tile([P, 2, 4, E], BF16, tag="hsrt", bufs=3, name="hsrt_%d" % c)
+        def passes1(c_list, g_lists):
+            for c in c_list:
+                state[("acc", c)] = [
+                    psum.tile([P, NC], F32, tag="acc", bufs=4, name="acc1_%d_%d" % (c, h)) for h in range(2)
+                ]
+                state[("pre", c)] = work.tile([P, 2, 4, E], F32, tag="pre", bufs=4, name="pre_%d" % c)
+                state[("hsrt", c)] = work.tile([P, 2, 4, E], BF16, tag="hsrt", bufs=4, name="hsrt_%d" % c)
+            for g_list in g_lists:
+                for c in c_list:
+                    for h in range(2):
+                        for g in g_list:
+                            mx1(state[("acc", c)][h], c, h, g)
+
+        def chain1(c_list):
+            for c in c_list:
+                add1(c, 0)
+                add1(c, 1)
+            for c in c_list:
+                silu1(c, 0)
+                silu1(c, 1)
+            for c in c_list:
+                mult1(c, 0)
+                mult1(c, 1)
 
         def add1(c, h):
             nc.vector.tensor_tensor(
@@ -234,7 +250,7 @@ def tile_node_interaction_w_kernel(
 
         def finish2(accs, n0, n1):
             w = n1 - n0
-            pre = work.tile([P, 2, NC], F32, tag="pre", name="pre2_%d" % n0)
+            pre = work.tile([P, 2, NC], F32, tag="pre", bufs=4, name="pre2_%d" % n0)
             for h in range(2):
                 nc.vector.tensor_tensor(out=pre[:, h, 0:w], in0=accs[h][:], in1=b2bc[:, n0:n1], op=ALU.add)
                 nc.scalar.activation(out=pre[:, h, 0:w], in_=pre[:, h, 0:w], func=ACT.Silu)
@@ -242,28 +258,32 @@ def tile_node_interaction_w_kernel(
             nc.vector.tensor_tensor(out=res[:, 0:w], in0=pre[:, 0, 0:w], in1=pre[:, 1, 0:w], op=ALU.add)
             nc.sync.dma_start(out=out2d[:, n0:n1], in_=res[:, 0:w])
 
-        for idx in range(4):
+        spread(1, 0)
+        spread(1, 1)
+        passes1((0,), ((0, 1), (2, 3)))
+        for idx in range(2, 6):
             spread(1, idx)
-        for i in range(G2):
-            passes1(i)
+        chain1((0,))
+        passes1((1,), ((0, 1, 2, 3),))
+        spread(1, 6)
+        spread(1, 7)
+        for idx in range(4):
+            spread(2, idx)
+        chain1((1,))
+        for i in range(1, 4):
+            passes1((2 * i, 2 * i + 1), ((0, 1), (2, 3)))
             if i >= 2:
-                flip(i - 2)
-            add1(i, 0)
-            if i >= 3:
-                quant(i - 3)
-            add1(i, 1)
-            silu1(i, 0)
-            silu1(i, 1)
-            mult1(i, 0)
-            mult1(i, 1)
-            if i >= 2:
-                copyout(i - 2)
-            if i == 0:
-                for idx in range(4, 8):
-                    spread(1, idx)
-            if i == 1:
-                for idx in range(4):
-                    spread(2, idx)
+                copyout(2 * i - 4)
+                copyout(2 * i - 3)
+                quant(2 * i - 4)
+                quant(2 * i - 3)
+            flip(2 * i - 2)
+            flip(2 * i - 1)
+            chain1((2 * i, 2 * i + 1))
+        copyout(4)
+        copyout(5)
+        quant(4)
+        quant(5)
 
         blk0 = [
             (psum.tile([P, NC], F32, tag="acc", bufs=4, name="acc2_%d_%d" % (j, h)), h, NC * j)
@@ -279,10 +299,9 @@ def tile_node_interaction_w_kernel(
         blk0_passes((0, 1))
         flip(6)
         flip(7)
-        quant(5)
         copyout(6)
-        quant(6)
         copyout(7)
+        quant(6)
         quant(7)
         blk0_passes((2, 3))
         blk0_passes((4, 5))
@@ -303,8 +322,9 @@ def tile_node_interaction_w_kernel(
         finish2(blk1, 1024, 1536)
 
         blk3 = [psum.tile([P, 256], F32, tag="acc", bufs=4, name="acc2d_%d" % h) for h in range(2)]
-        for h in range(2):
-            for g in range(G2):
-                mx2(blk3[h], h, g, 1792, 2048)
+        for g_list in ((0, 1, 2, 3), (4, 5, 6, 7)):
+            for h in range(2):
+                for g in g_list:
+                    mx2(blk3[h], h, g, 1792, 2048)
         finish2(blk2, 1536, 1792)
         finish2(blk3, 1792, 2048)

@@ -45,7 +45,8 @@ def tile_node_interaction_w_kernel(
         xs = keep.tile([P, G1, 2 * E], U8, align_bytes=64)
         hq = keep.tile([P, G2, 2 * E], U32, align_bytes=64)
         hs = keep.tile([P, G2, 2 * E], U8, align_bytes=64)
-        b1z = keep.tile([P, H], BF16, align_bytes=64)
+        b1za = keep.tile([P, H // 2], BF16, align_bytes=64)
+        b1zb = keep.tile([P, H // 2], BF16, align_bytes=64)
         b2z = keep.tile([P, D], BF16, align_bytes=64)
         b1bc = keep.tile([P, G2, 4, E], BF16)
         b2bc = keep.tile([P, D], BF16)
@@ -53,12 +54,14 @@ def tile_node_interaction_w_kernel(
         identb = keep.tile([P, P], BF16)
         ones = keep.tile([P, P], BF16)
 
-        nc.vector.memset(b1z[:].bitcast(I32), 0)
+        nc.vector.memset(b1za[:].bitcast(I32), 0)
         nc.vector.memset(planes1[:].bitcast(I32), 0)
-        nc.vector.memset(planes2[:].rearrange("p a n -> p (a n)").bitcast(I32), 0)
+        nc.vector.memset(b1zb[:].bitcast(I32), 0)
         nc.vector.memset(b2z[:].bitcast(I32), 0)
+        nc.vector.memset(planes2[:].rearrange("p a n -> p (a n)").bitcast(I32), 0)
         nc.gpsimd.memset(ones[:], 1.0)
         make_identity(nc, identf[:])
+        make_identity(nc, identb[:])
 
         w1v = W1_words.rearrange("g p n t -> g p (n t)").bitcast(I32)
         w2v = W2_words.rearrange("g p n t -> g p (n t)").bitcast(I32)
@@ -83,16 +86,24 @@ def tile_node_interaction_w_kernel(
                     in_=s1v[:, 4 * q : 4 * q + 4, n0 // 4 : n1 // 4],
                 )
 
-        nc.scalar.dma_start(out=b1z[0:1, :], in_=b1.rearrange("(o n) -> o n", o=1))
+        b1row = b1.rearrange("(o n) -> o n", o=1)
+        nc.scalar.dma_start(out=b1za[0:1, :], in_=b1row[:, 0 : H // 2])
+        nc.scalar.dma_start(out=b1zb[0:1, :], in_=b1row[:, H // 2 : H])
+        nc.scalar.dma_start(out=b2z[0:1, :], in_=b2.rearrange("(o n) -> o n", o=1))
         nc.sync.dma_start(out=x_sb[:, 0, :], in_=node_embed)
         nc.sync.dma_start(out=x_sb[:, 1, :], in_=ori)
-        load_s1(0, 1024)
+        load_s1(0, 4096)
+        s2v = W2_scales.bitcast(I32)
+        for a in range(2):
+            for q in range(4):
+                nc.sync.dma_start(
+                    out=planes2[32 * q : 32 * q + 16, a, :].bitcast(I32),
+                    in_=s2v[4 * a : 4 * a + 4, 4 * q : 4 * q + 4, :],
+                )
         load_w1(0, 2, 0, 512)
         load_w1(2, 4, 0, 512)
         load_w1(0, 4, 512, 1024)
         nc.sync.dma_start(out=xe_sb[:, 0:1024], in_=x_edge_c[:, 0:1024])
-        nc.sync.dma_start(out=b2z[0:1, :], in_=b2.rearrange("(o n) -> o n", o=1))
-        load_s1(1024, 4096)
         load_w1(0, 2, 1024, 2048)
         load_w1(2, 4, 1024, 2048)
         nc.sync.dma_start(out=xe_sb[:, 1024:4096], in_=x_edge_c[:, 1024:4096])
@@ -100,14 +111,6 @@ def tile_node_interaction_w_kernel(
         load_w1(2, 4, 2048, 3072)
         load_w1(0, 2, 3072, 4096)
         load_w1(2, 4, 3072, 4096)
-        s2f = W2_scales.bitcast(F32)
-        for a in range(2):
-            for q in range(4):
-                nc.gpsimd.dma_start(
-                    out=planes2[32 * q : 32 * q + 16, a, :].bitcast(F32),
-                    in_=s2f[4 * a : 4 * a + 4, 4 * q : 4 * q + 4, :],
-                )
-        make_identity(nc, identb[:])
         for gp in range(4):
             load_w2(2 * gp, 2 * gp + 2, 0, 1024)
         load_w2(0, 4, 1024, 1536)
@@ -116,46 +119,43 @@ def tile_node_interaction_w_kernel(
         load_w2(0, 4, 1792, 2048)
         load_w2(4, 8, 1792, 2048)
 
-        xts = []
-        for g in range(G1):
-            xT = psum.tile([P, 2, 2, E], F32, tag="acc", bufs=4, name="xT_%d" % g)
-            for h in range(2):
-                xw = x_sb[:, h, :].bitcast(F32)
-                for u in range(2):
-                    nc.tensor.transpose(xT[:, h, u, :], xw[:, 256 * g + u : 256 * (g + 1) : 2], identf[:])
-            xts.append(xT)
-        for g in (0, 2, 1, 3):
-            dst = xg[:, g].bitcast(F32)
-            src = xts[g][:].rearrange("p h u r -> p h r u")
-            if g % 2 == 0:
-                nc.vector.tensor_copy(out=dst, in_=src)
-            else:
-                nc.scalar.copy(out=dst, in_=src)
-        for g in range(G1):
-            nc.vector.quantize_mx(
-                out=xq[:, g, :].bitcast(FP8X4),
-                scales=xs[:, g, :],
-                in_=xg[:, g].rearrange("p h r t -> p (h r t)"),
-            )
-
         bc_count = [0]
 
         def spread(which, idx):
             k = bc_count[0]
             bc_count[0] = k + 1
             bps = psum.tile([P, NC], F32, tag=("mi" if k % 4 < 2 else "tp"), name="bps_%d" % k)
-            src_z = b1z if which == 1 else b2z
-            nc.tensor.matmul(out=bps[:], lhsT=ones[:], rhs=src_z[:, NC * idx : NC * (idx + 1)], start=True, stop=True)
+            src_z = b2z if which == 2 else (b1za if idx < 4 else b1zb)
+            col = NC * (idx % 4)
+            nc.tensor.matmul(out=bps[:], lhsT=ones[:], rhs=src_z[:, col : col + NC], start=True, stop=True)
             if which == 1:
-                dst = b1bc[:, idx]
-                src = bps[:].rearrange("p (q t) -> p t q", t=4)
+                nc.scalar.copy(out=b1bc[:, idx], in_=bps[:].rearrange("p (q t) -> p t q", t=4))
             else:
-                dst = b2bc[:, NC * idx : NC * (idx + 1)]
-                src = bps[:]
-            if k % 2 == 0:
-                nc.scalar.copy(out=dst, in_=src)
-            else:
-                nc.vector.tensor_copy(out=dst, in_=src)
+                nc.scalar.copy(out=b2bc[:, NC * idx : NC * (idx + 1)], in_=bps[:])
+
+        for idx in range(4):
+            spread(1, idx)
+
+        def quant_x(g):
+            nc.vector.quantize_mx(
+                out=xq[:, g, :].bitcast(FP8X4),
+                scales=xs[:, g, :],
+                in_=xg[:, g].rearrange("p h r t -> p (h r t)"),
+            )
+
+        for g in range(G1):
+            xT = psum.tile([P, 2, 2, E], F32, tag="acc", bufs=4, name="xT_%d" % g)
+            for h in range(2):
+                xw = x_sb[:, h, :].bitcast(F32)
+                for u in range(2):
+                    nc.tensor.transpose(xT[:, h, u, :], xw[:, 256 * g + u : 256 * (g + 1) : 2], identf[:])
+            nc.vector.tensor_copy(out=xg[:, g].bitcast(F32), in_=xT[:].rearrange("p h u r -> p h r u"))
+            if g >= 1:
+                quant_x(g - 1)
+            spread(1, 4 + g)
+        quant_x(G1 - 1)
+        for idx in range(4):
+            spread(2, idx)
 
         state = {}
 
@@ -258,17 +258,9 @@ def tile_node_interaction_w_kernel(
             nc.vector.tensor_tensor(out=res[:, 0:w], in0=pre[:, 0, 0:w], in1=pre[:, 1, 0:w], op=ALU.add)
             nc.sync.dma_start(out=out2d[:, n0:n1], in_=res[:, 0:w])
 
-        spread(1, 0)
-        spread(1, 1)
         passes1((0,), ((0, 1), (2, 3)))
-        for idx in range(2, 6):
-            spread(1, idx)
         chain1((0,))
         passes1((1,), ((0, 1, 2, 3),))
-        spread(1, 6)
-        spread(1, 7)
-        for idx in range(4):
-            spread(2, idx)
         chain1((1,))
         for i in range(1, 4):
             passes1((2 * i, 2 * i + 1), ((0, 1), (2, 3)))

@@ -191,8 +191,7 @@ def tile_node_interaction_w_kernel(
                 silu1(c, 0)
                 silu1(c, 1)
             for c in c_list:
-                mult1(c, 0)
-                mult1(c, 1)
+                mult1(c)
 
         def add1(c, h):
             nc.vector.tensor_tensor(
@@ -206,12 +205,14 @@ def tile_node_interaction_w_kernel(
             pre = state[("pre", c)]
             nc.scalar.activation(out=pre[:, h], in_=pre[:, h], func=ACT.Silu)
 
-        def mult1(c, h):
-            eng = nc.vector if h == 0 else nc.gpsimd
-            eng.tensor_tensor(
-                out=state[("hsrt", c)][:, h],
-                in0=state[("pre", c)][:, h],
-                in1=xe_sb[:, NC * c : NC * (c + 1)].rearrange("p (q t) -> p t q", t=4),
+        def mult1(c):
+            nc.vector.tensor_tensor(
+                out=state[("hsrt", c)][:],
+                in0=state[("pre", c)][:],
+                in1=xe_sb[:, NC * c : NC * (c + 1)]
+                .rearrange("p (q t) -> p t q", t=4)
+                .unsqueeze(1)
+                .to_broadcast([P, 2, 4, E]),
                 op=ALU.mult,
             )
 

@@ -9,18 +9,26 @@ I32 = mybir.dt.int32
 U32 = mybir.dt.uint32
 U8 = mybir.dt.uint8
 FP8X4 = mybir.dt.float8_e4m3fn_x4
-ACT = mybir.ActivationFunctionType
-ALU = mybir.AluOpType
+SILU = mybir.ActivationFunctionType.Silu
+ADD = mybir.AluOpType.add
+MULT = mybir.AluOpType.mult
 
 P = 128
 E = 128
+HALVES = 2
 D = 2048
 H = 4096
-G1 = D // 512
-G2 = H // 512
-NC = 512
+PACK = 4
+K_PASS = P * PACK
+G1 = D // K_PASS
+G2 = H // K_PASS
+CHUNK = 512
+PAIRS = H // (2 * CHUNK)
+PLANES = 4
 
-FLOPS = 2 * (2 * E) * D * H * 2
+BLOCKS = ((0, 2, 512, 2), (1024, 1, 512, 4), (1536, 1, 256, 8), (1792, 1, 256, 4))
+
+FLOPS = 2 * (HALVES * E) * D * H * 2
 
 
 def tile_node_interaction_w_kernel(
@@ -32,292 +40,226 @@ def tile_node_interaction_w_kernel(
         ctx.enter_context(tc.manual_schedule())
         keep = ctx.enter_context(tc.tile_pool(name="keep", bufs=1))
         work = ctx.enter_context(tc.tile_pool(name="work", bufs=2))
-        psum = ctx.enter_context(tc.psum_pool(name="psum", bufs=2))
+        psum = ctx.enter_context(tc.psum_pool(name="psum", bufs=4))
 
-        w1_sb = keep.tile([P, G1, H], U32, align_bytes=64)
-        w2_sb = keep.tile([P, G2, D], U32, align_bytes=64)
-        planes1 = keep.tile([P, H], U8, align_bytes=64)
-        planes2 = keep.tile([P, 2, D], U8, align_bytes=64)
-        x_sb = keep.tile([P, 2, D], BF16, align_bytes=64)
-        xe_sb = keep.tile([P, H], BF16, align_bytes=64)
-        xg = keep.tile([P, G1, 2, E, 4], BF16, align_bytes=64)
-        xq = keep.tile([P, G1, 2 * E], U32, align_bytes=64)
-        xs = keep.tile([P, G1, 2 * E], U8, align_bytes=64)
-        hq = keep.tile([P, G2, 2 * E], U32, align_bytes=64)
-        hs = keep.tile([P, G2, 2 * E], U8, align_bytes=64)
-        b1za = keep.tile([P, H // 2], BF16, align_bytes=64)
-        b1zb = keep.tile([P, H // 2], BF16, align_bytes=64)
-        b2z = keep.tile([P, D], BF16, align_bytes=64)
-        b1bc = keep.tile([P, G2, 4, E], BF16)
-        b2bc = keep.tile([P, D], BF16)
-        identf = keep.tile([P, P], F32)
-        identb = keep.tile([P, P], BF16)
+        w1_words = keep.tile([P, G1, H], U32, align_bytes=64)
+        w2_words = keep.tile([P, G2, D], U32, align_bytes=64)
+        w1_planes = keep.tile([P, H], U8, align_bytes=64)
+        w2_planes = keep.tile([P, G2 // PLANES, D], U8, align_bytes=64)
+        x_rows = keep.tile([P, HALVES, D], BF16, align_bytes=64)
+        gate = keep.tile([P, H], BF16, align_bytes=64)
+        x_grouped = keep.tile([P, G1, HALVES, E, PACK], BF16, align_bytes=64)
+        x_words = keep.tile([P, G1, HALVES * E], U32, align_bytes=64)
+        x_planes = keep.tile([P, G1, HALVES * E], U8, align_bytes=64)
+        h_words = keep.tile([P, G2, HALVES * E], U32, align_bytes=64)
+        h_planes = keep.tile([P, G2, HALVES * E], U8, align_bytes=64)
+        bias_row = keep.tile([P, H + D], BF16, align_bytes=64)
+        bias_all = keep.tile([P, H + D], BF16)
+        ident_f32 = keep.tile([P, P], F32)
+        ident_bf16 = keep.tile([P, P], BF16)
         ones = keep.tile([P, P], BF16)
 
-        nc.vector.memset(b1za[:].bitcast(I32), 0)
-        nc.vector.memset(planes1[:].bitcast(I32), 0)
-        nc.vector.memset(b1zb[:].bitcast(I32), 0)
-        nc.vector.memset(b2z[:].bitcast(I32), 0)
-        nc.vector.memset(planes2[:].rearrange("p a n -> p (a n)").bitcast(I32), 0)
+        nc.vector.memset(bias_row[:].bitcast(I32), 0)
+        nc.vector.memset(w1_planes[:].bitcast(I32), 0)
+        nc.vector.memset(w2_planes[:].rearrange("p a n -> p (a n)").bitcast(I32), 0)
         nc.gpsimd.memset(ones[:], 1.0)
-        make_identity(nc, identf[:])
-        make_identity(nc, identb[:])
+        make_identity(nc, ident_f32[:])
+        make_identity(nc, ident_bf16[:])
 
-        w1v = W1_words.rearrange("g p n t -> g p (n t)").bitcast(I32)
-        w2v = W2_words.rearrange("g p n t -> g p (n t)").bitcast(I32)
-        s1v = W1_scales.bitcast(I32)
+        w1_dram = W1_words.rearrange("g p n t -> g p (n t)").bitcast(I32)
+        w2_dram = W2_words.rearrange("g p n t -> g p (n t)").bitcast(I32)
+        s1_dram = W1_scales.bitcast(I32)
+        s2_dram = W2_scales.bitcast(I32)
 
-        def load_w1(g0, g1, n0, n1):
+        def load_words(sbuf, dram, g0, g1, n0, n1):
             nc.sync.dma_start(
-                out=w1_sb[:, g0:g1, n0:n1].bitcast(I32),
-                in_=w1v[g0:g1, :, n0:n1].rearrange("g p n -> p g n"),
+                out=sbuf[:, g0:g1, n0:n1].bitcast(I32),
+                in_=dram[g0:g1, :, n0:n1].rearrange("g p n -> p g n"),
             )
 
-        def load_w2(g0, g1, n0, n1):
+        nc.scalar.dma_start(out=bias_row[0:1, 0:H], in_=b1.rearrange("(o n) -> o n", o=1))
+        nc.scalar.dma_start(out=bias_row[0:1, H : H + D], in_=b2.rearrange("(o n) -> o n", o=1))
+        nc.sync.dma_start(out=x_rows[:, 0, :], in_=node_embed)
+        nc.sync.dma_start(out=x_rows[:, 1, :], in_=ori)
+        for quad in range(4):
             nc.sync.dma_start(
-                out=w2_sb[:, g0:g1, n0:n1].bitcast(I32),
-                in_=w2v[g0:g1, :, n0:n1].rearrange("g p n -> p g n"),
+                out=w1_planes[32 * quad : 32 * quad + 16, :].bitcast(I32),
+                in_=s1_dram[:, 4 * quad : 4 * quad + 4, :],
             )
-
-        def load_s1(n0, n1):
-            for q in range(4):
+        for a in range(G2 // PLANES):
+            for quad in range(4):
                 nc.sync.dma_start(
-                    out=planes1[32 * q : 32 * q + 16, n0:n1].bitcast(I32),
-                    in_=s1v[:, 4 * q : 4 * q + 4, n0 // 4 : n1 // 4],
+                    out=w2_planes[32 * quad : 32 * quad + 16, a, :].bitcast(I32),
+                    in_=s2_dram[PLANES * a : PLANES * (a + 1), 4 * quad : 4 * quad + 4, :],
                 )
+        for pair in range(PAIRS):
+            for g in range(G1):
+                load_words(w1_words, w1_dram, g, g + 1, 2 * CHUNK * pair, 2 * CHUNK * (pair + 1))
+            if pair == 0:
+                nc.sync.dma_start(out=gate[:], in_=x_edge_c)
+        for first, chunks, width, k_cut in BLOCKS:
+            for g0 in range(0, G2, k_cut):
+                load_words(w2_words, w2_dram, g0, g0 + k_cut, first, first + chunks * width)
 
-        b1row = b1.rearrange("(o n) -> o n", o=1)
-        nc.scalar.dma_start(out=b1za[0:1, :], in_=b1row[:, 0 : H // 2])
-        nc.scalar.dma_start(out=b1zb[0:1, :], in_=b1row[:, H // 2 : H])
-        nc.scalar.dma_start(out=b2z[0:1, :], in_=b2.rearrange("(o n) -> o n", o=1))
-        nc.sync.dma_start(out=x_sb[:, 0, :], in_=node_embed)
-        nc.sync.dma_start(out=x_sb[:, 1, :], in_=ori)
-        load_s1(0, 4096)
-        s2v = W2_scales.bitcast(I32)
-        for a in range(2):
-            for q in range(4):
-                nc.sync.dma_start(
-                    out=planes2[32 * q : 32 * q + 16, a, :].bitcast(I32),
-                    in_=s2v[4 * a : 4 * a + 4, 4 * q : 4 * q + 4, :],
-                )
-        load_w1(0, 2, 0, 512)
-        load_w1(2, 4, 0, 512)
-        load_w1(0, 4, 512, 1024)
-        nc.sync.dma_start(out=xe_sb[:, 0:1024], in_=x_edge_c[:, 0:1024])
-        load_w1(0, 2, 1024, 2048)
-        load_w1(2, 4, 1024, 2048)
-        nc.sync.dma_start(out=xe_sb[:, 1024:4096], in_=x_edge_c[:, 1024:4096])
-        load_w1(0, 2, 2048, 3072)
-        load_w1(2, 4, 2048, 3072)
-        load_w1(0, 2, 3072, 4096)
-        load_w1(2, 4, 3072, 4096)
-        for gp in range(4):
-            load_w2(2 * gp, 2 * gp + 2, 0, 1024)
-        load_w2(0, 4, 1024, 1536)
-        load_w2(4, 8, 1024, 1536)
-        load_w2(0, 8, 1536, 1792)
-        load_w2(0, 4, 1792, 2048)
-        load_w2(4, 8, 1792, 2048)
-
-        bc_count = [0]
-
-        def spread(which, idx):
-            k = bc_count[0]
-            bc_count[0] = k + 1
-            bps = psum.tile([P, NC], F32, tag=("mi" if k % 4 < 2 else "tp"), name="bps_%d" % k)
-            src_z = b2z if which == 2 else (b1za if idx < 4 else b1zb)
-            col = NC * (idx % 4)
-            nc.tensor.matmul(out=bps[:], lhsT=ones[:], rhs=src_z[:, col : col + NC], start=True, stop=True)
-            if which == 1:
-                nc.scalar.copy(out=b1bc[:, idx], in_=bps[:].rearrange("p (q t) -> p t q", t=4))
-            else:
-                nc.scalar.copy(out=b2bc[:, NC * idx : NC * (idx + 1)], in_=bps[:])
-
-        for idx in range(4):
-            spread(1, idx)
-
-        def quant_x(g):
+        def quantise_x(g):
             nc.vector.quantize_mx(
-                out=xq[:, g, :].bitcast(FP8X4),
-                scales=xs[:, g, :],
-                in_=xg[:, g].rearrange("p h r t -> p (h r t)"),
+                out=x_words[:, g, :].bitcast(FP8X4),
+                scales=x_planes[:, g, :],
+                in_=x_grouped[:, g].rearrange("p h r t -> p (h r t)"),
             )
 
         for g in range(G1):
-            xT = psum.tile([P, 2, 2, E], F32, tag="acc", bufs=4, name="xT_%d" % g)
-            for h in range(2):
-                xw = x_sb[:, h, :].bitcast(F32)
+            x_t = psum.tile([P, HALVES, 2, E], F32, tag="acc", name="x_t_%d" % g)
+            for h in range(HALVES):
+                pairs_of_k = x_rows[:, h, :].bitcast(F32)
                 for u in range(2):
-                    nc.tensor.transpose(xT[:, h, u, :], xw[:, 256 * g + u : 256 * (g + 1) : 2], identf[:])
-            nc.vector.tensor_copy(out=xg[:, g].bitcast(F32), in_=xT[:].rearrange("p h u r -> p h r u"))
+                    nc.tensor.transpose(
+                        x_t[:, h, u, :], pairs_of_k[:, 256 * g + u : 256 * (g + 1) : 2], ident_f32[:]
+                    )
+            nc.vector.tensor_copy(
+                out=x_grouped[:, g].bitcast(F32), in_=x_t[:].rearrange("p h u r -> p h r u")
+            )
             if g >= 1:
-                quant_x(g - 1)
-            spread(1, 4 + g)
-        quant_x(G1 - 1)
-        for idx in range(4):
-            spread(2, idx)
+                quantise_x(g - 1)
+        quantise_x(G1 - 1)
 
-        state = {}
+        for k in range((H + D) // (2 * CHUNK)):
+            spread = psum.tile([P, 2 * CHUNK], BF16, tag="side", name="spread_%d" % k)
+            for j in range(2):
+                nc.tensor.matmul(
+                    out=spread[:, CHUNK * j : CHUNK * (j + 1)],
+                    lhsT=ones[:],
+                    rhs=bias_row[:, CHUNK * (2 * k + j) : CHUNK * (2 * k + j + 1)],
+                    start=True,
+                    stop=True,
+                )
+            nc.scalar.copy(out=bias_all[:, 2 * CHUNK * k : 2 * CHUNK * (k + 1)], in_=spread[:])
 
-        def mx1(acc, c, h, g):
-            nc.tensor.matmul_mx(
-                out=acc[:],
-                lhsT=xq[:, g, E * h : E * (h + 1)].bitcast(FP8X4),
-                lhsT_scale=xs[:, g, E * h : E * (h + 1)],
-                rhs=w1_sb[:, g, NC * c : NC * (c + 1)].bitcast(FP8X4),
-                rhs_scale=planes1[4 * g : P, NC * c : NC * (c + 1)],
-                start=(g == 0),
-                stop=(g == G1 - 1),
-            )
+        sums1 = {}
+        acts = {}
+        h_sorted = {}
+        h_t = {}
+        h_grouped = {}
 
-        def passes1(c_list, g_lists):
-            for c in c_list:
-                state[("acc", c)] = [
-                    psum.tile([P, NC], F32, tag="acc", bufs=4, name="acc1_%d_%d" % (c, h)) for h in range(2)
-                ]
-                state[("pre", c)] = work.tile([P, 2, 4, E], F32, tag="pre", bufs=4, name="pre_%d" % c)
-                state[("hsrt", c)] = work.tile([P, 2, 4, E], BF16, tag="hsrt", bufs=4, name="hsrt_%d" % c)
-            for g_list in g_lists:
-                for c in c_list:
-                    for h in range(2):
-                        for g in g_list:
-                            mx1(state[("acc", c)][h], c, h, g)
+        def by_t(columns):
+            return columns.rearrange("p (q t) -> p t q", t=PACK)
 
-        def chain1(c_list):
-            for c in c_list:
-                add1(c, 0)
-                add1(c, 1)
-            for c in c_list:
-                silu1(c, 0)
-                silu1(c, 1)
-            for c in c_list:
-                mult1(c)
+        def passes1(pair):
+            chunks = (2 * pair, 2 * pair + 1)
+            for c in chunks:
+                for h in range(HALVES):
+                    sums1[(c, h)] = psum.tile([P, CHUNK], F32, tag="acc", name="sums1_%d_%d" % (c, h))
+                acts[c] = work.tile([P, HALVES, PACK, E], F32, tag="acts", bufs=4, name="acts_%d" % c)
+                h_sorted[c] = work.tile([P, HALVES, PACK, E], BF16, tag="h_sorted", bufs=4, name="h_sorted_%d" % c)
+            for g in range(G1):
+                for c in chunks:
+                    for h in range(HALVES):
+                        nc.tensor.matmul_mx(
+                            out=sums1[(c, h)][:],
+                            lhsT=x_words[:, g, E * h : E * (h + 1)].bitcast(FP8X4),
+                            lhsT_scale=x_planes[:, g, E * h : E * (h + 1)],
+                            rhs=w1_words[:, g, CHUNK * c : CHUNK * (c + 1)].bitcast(FP8X4),
+                            rhs_scale=w1_planes[4 * g : P, CHUNK * c : CHUNK * (c + 1)],
+                            start=(g == 0),
+                            stop=(g == G1 - 1),
+                        )
 
-        def add1(c, h):
-            nc.vector.tensor_tensor(
-                out=state[("pre", c)][:, h],
-                in0=state[("acc", c)][h][:].rearrange("p (q t) -> p t q", t=4),
-                in1=b1bc[:, c],
-                op=ALU.add,
-            )
+        def activate(pair):
+            chunks = (2 * pair, 2 * pair + 1)
+            for c in chunks:
+                for h in range(HALVES):
+                    nc.vector.tensor_tensor(
+                        out=acts[c][:, h],
+                        in0=by_t(sums1[(c, h)][:]),
+                        in1=by_t(bias_all[:, CHUNK * c : CHUNK * (c + 1)]),
+                        op=ADD,
+                    )
+            for c in chunks:
+                for h in range(HALVES):
+                    nc.scalar.activation(out=acts[c][:, h], in_=acts[c][:, h], func=SILU)
+            for c in chunks:
+                nc.vector.tensor_tensor(
+                    out=h_sorted[c][:],
+                    in0=acts[c][:],
+                    in1=by_t(gate[:, CHUNK * c : CHUNK * (c + 1)]).unsqueeze(1).to_broadcast([P, HALVES, PACK, E]),
+                    op=MULT,
+                )
 
-        def silu1(c, h):
-            pre = state[("pre", c)]
-            nc.scalar.activation(out=pre[:, h], in_=pre[:, h], func=ACT.Silu)
+        def transpose_h(pair):
+            for c in (2 * pair, 2 * pair + 1):
+                h_t[c] = psum.tile([P, HALVES, PACK, E], BF16, tag="side", name="h_t_%d" % c)
+                for h in range(HALVES):
+                    for t in range(PACK):
+                        nc.tensor.transpose(h_t[c][:, h, t, :], h_sorted[c][:, h, t, :], ident_bf16[:])
 
-        def mult1(c):
-            nc.vector.tensor_tensor(
-                out=state[("hsrt", c)][:],
-                in0=state[("pre", c)][:],
-                in1=xe_sb[:, NC * c : NC * (c + 1)]
-                .rearrange("p (q t) -> p t q", t=4)
-                .unsqueeze(1)
-                .to_broadcast([P, 2, 4, E]),
-                op=ALU.mult,
-            )
+        def quantise_h(pair):
+            chunks = (2 * pair, 2 * pair + 1)
+            for c in chunks:
+                h_grouped[c] = work.tile([P, HALVES, E, PACK], BF16, tag="h_grouped", name="h_grouped_%d" % c, align_bytes=64)
+                nc.scalar.copy(out=h_grouped[c][:], in_=h_t[c][:].rearrange("p h t r -> p h r t"))
+            for c in chunks:
+                nc.vector.quantize_mx(
+                    out=h_words[:, c, :].bitcast(FP8X4),
+                    scales=h_planes[:, c, :],
+                    in_=h_grouped[c][:].rearrange("p h r t -> p (h r t)"),
+                )
 
-        def flip(c):
-            hsrt = state[("hsrt", c)]
-            tp = psum.tile([P, 2, 4, E], BF16, tag="tp", name="tp_%d" % c)
-            for h in range(2):
-                for t in range(4):
-                    nc.tensor.transpose(tp[:, h, t, :], hsrt[:, h, t, :], identb[:])
-            state[("tp", c)] = tp
+        for pair in range(PAIRS):
+            passes1(pair)
+            if pair >= 2:
+                quantise_h(pair - 2)
+            if pair >= 1:
+                transpose_h(pair - 1)
+            activate(pair)
+        quantise_h(PAIRS - 2)
 
-        def copyout(c):
-            hg = work.tile([P, 2, E, 4], BF16, tag="hg", name="hg_%d" % c, align_bytes=64)
-            nc.scalar.copy(out=hg[:], in_=state[("tp", c)][:].rearrange("p h t r -> p h r t"))
-            state[("hg", c)] = hg
+        out_rows = out.rearrange("e a c -> e (a c)")
 
-        def quant(c):
-            nc.vector.quantize_mx(
-                out=hq[:, c, :].bitcast(FP8X4),
-                scales=hs[:, c, :],
-                in_=state[("hg", c)][:].rearrange("p h r t -> p (h r t)"),
-            )
+        def open2(block, ring):
+            first, chunks, width, k_cut = block
+            return [
+                (psum.tile([P, width], F32, tag=ring, name="sums2_%d_%d" % (first + width * j, h)), h, first + width * j)
+                for j in range(chunks)
+                for h in range(HALVES)
+            ]
 
-        def mx2(acc, h, g, n0, n1):
-            nc.tensor.matmul_mx(
-                out=acc[:],
-                lhsT=hq[:, g, E * h : E * (h + 1)].bitcast(FP8X4),
-                lhsT_scale=hs[:, g, E * h : E * (h + 1)],
-                rhs=w2_sb[:, g, n0:n1].bitcast(FP8X4),
-                rhs_scale=planes2[4 * (g % 4) : P, g // 4, n0:n1],
-                start=(g == 0),
-                stop=(g == G2 - 1),
-            )
+        def passes2(sums, width, g0, g1):
+            for acc, h, n0 in sums:
+                for g in range(g0, g1):
+                    nc.tensor.matmul_mx(
+                        out=acc[:],
+                        lhsT=h_words[:, g, E * h : E * (h + 1)].bitcast(FP8X4),
+                        lhsT_scale=h_planes[:, g, E * h : E * (h + 1)],
+                        rhs=w2_words[:, g, n0 : n0 + width].bitcast(FP8X4),
+                        rhs_scale=w2_planes[4 * (g % PLANES) : P, g // PLANES, n0 : n0 + width],
+                        start=(g == 0),
+                        stop=(g == G2 - 1),
+                    )
 
-        out2d = out.rearrange("e a c -> e (a c)")
+        def finish2(sums, width):
+            for j in range(len(sums) // HALVES):
+                n0 = sums[HALVES * j][2]
+                y = work.tile([P, HALVES, CHUNK], F32, tag="acts", bufs=4, name="y_%d" % n0)
+                for acc, h, n0_same in sums[HALVES * j : HALVES * (j + 1)]:
+                    nc.vector.tensor_tensor(
+                        out=y[:, h, 0:width], in0=acc[:], in1=bias_all[:, H + n0 : H + n0 + width], op=ADD
+                    )
+                    nc.scalar.activation(out=y[:, h, 0:width], in_=y[:, h, 0:width], func=SILU)
+                both = work.tile([P, CHUNK], F32, tag="both", name="both_%d" % n0)
+                nc.vector.tensor_tensor(out=both[:, 0:width], in0=y[:, 0, 0:width], in1=y[:, 1, 0:width], op=ADD)
+                nc.sync.dma_start(out=out_rows[:, n0 : n0 + width], in_=both[:, 0:width])
 
-        def finish2(accs, n0, n1):
-            w = n1 - n0
-            pre = work.tile([P, 2, NC], F32, tag="pre", bufs=4, name="pre2_%d" % n0)
-            for h in range(2):
-                nc.vector.tensor_tensor(out=pre[:, h, 0:w], in0=accs[h][:], in1=b2bc[:, n0:n1], op=ALU.add)
-                nc.scalar.activation(out=pre[:, h, 0:w], in_=pre[:, h, 0:w], func=ACT.Silu)
-            res = work.tile([P, NC], F32, tag="res", name="res_%d" % n0)
-            nc.vector.tensor_tensor(out=res[:, 0:w], in0=pre[:, 0, 0:w], in1=pre[:, 1, 0:w], op=ALU.add)
-            nc.sync.dma_start(out=out2d[:, n0:n1], in_=res[:, 0:w])
-
-        passes1((0,), ((0, 1), (2, 3)))
-        chain1((0,))
-        passes1((1,), ((0, 1, 2, 3),))
-        chain1((1,))
-        for i in range(1, 4):
-            passes1((2 * i, 2 * i + 1), ((0, 1), (2, 3)))
-            if i >= 2:
-                copyout(2 * i - 4)
-                copyout(2 * i - 3)
-                quant(2 * i - 4)
-                quant(2 * i - 3)
-            flip(2 * i - 2)
-            flip(2 * i - 1)
-            chain1((2 * i, 2 * i + 1))
-        copyout(4)
-        copyout(5)
-        quant(4)
-        quant(5)
-
-        blk0 = [
-            (psum.tile([P, NC], F32, tag="acc", bufs=4, name="acc2_%d_%d" % (j, h)), h, NC * j)
-            for j in range(2)
-            for h in range(2)
-        ]
-
-        def blk0_passes(g_list):
-            for acc, h, n0 in blk0:
-                for g in g_list:
-                    mx2(acc, h, g, n0, n0 + NC)
-
-        blk0_passes((0, 1))
-        flip(6)
-        flip(7)
-        copyout(6)
-        copyout(7)
-        quant(6)
-        quant(7)
-        blk0_passes((2, 3))
-        blk0_passes((4, 5))
-        blk0_passes((6, 7))
-
-        blk1 = [psum.tile([P, NC], F32, tag="mi", name="acc2b_%d" % h) for h in range(2)]
-        for g_list in ((0, 1, 2, 3), (4, 5, 6, 7)):
-            for h in range(2):
-                for g in g_list:
-                    mx2(blk1[h], h, g, 1024, 1536)
-        finish2([blk0[0][0], blk0[1][0]], 0, 512)
-        finish2([blk0[2][0], blk0[3][0]], 512, 1024)
-
-        blk2 = [psum.tile([P, 256], F32, tag="tp", name="acc2c_%d" % h) for h in range(2)]
-        for h in range(2):
-            for g in range(G2):
-                mx2(blk2[h], h, g, 1536, 1792)
-        finish2(blk1, 1024, 1536)
-
-        blk3 = [psum.tile([P, 256], F32, tag="acc", bufs=4, name="acc2d_%d" % h) for h in range(2)]
-        for g_list in ((0, 1, 2, 3), (4, 5, 6, 7)):
-            for h in range(2):
-                for g in g_list:
-                    mx2(blk3[h], h, g, 1792, 2048)
-        finish2(blk2, 1536, 1792)
-        finish2(blk3, 1792, 2048)
+        rings = ("acc", "side", "side", "acc")
+        before = None
+        for block, ring in zip(BLOCKS, rings):
+            first, chunks, width, k_cut = block
+            sums = open2(block, ring)
+            for g0 in range(0, G2, k_cut):
+                passes2(sums, width, g0, g0 + k_cut)
+                if first == 0 and g0 == 0:
+                    transpose_h(PAIRS - 1)
+                    quantise_h(PAIRS - 1)
+            if before is not None:
+                finish2(before[0], before[1])
+            before = (sums, width)
+        finish2(before[0], before[1])

@@ -53,18 +53,16 @@ def tile_node_interaction_w_kernel(
         x_planes = keep.tile([P, G1, HALVES * E], U8, align_bytes=64)
         h_words = keep.tile([P, G2, HALVES * E], U32, align_bytes=64)
         h_planes = keep.tile([P, G2, HALVES * E], U8, align_bytes=64)
-        bias_row = keep.tile([P, H + D], BF16, align_bytes=64)
+        bias_rows = keep.tile([P, CHUNK], BF16, align_bytes=64)
         bias_all = keep.tile([P, H + D], BF16)
         ident_f32 = keep.tile([P, P], F32)
         ident_bf16 = keep.tile([P, P], BF16)
-        ones = keep.tile([P, P], BF16)
 
-        nc.vector.memset(bias_row[:].bitcast(I32), 0)
+        nc.vector.memset(bias_rows[:].bitcast(I32), 0)
         nc.vector.memset(w1_planes[:].bitcast(I32), 0)
         nc.vector.memset(w2_planes[:].rearrange("p a n -> p (a n)").bitcast(I32), 0)
-        nc.gpsimd.memset(ones[:], 1.0)
-        make_identity(nc, ident_f32[:])
         make_identity(nc, ident_bf16[:])
+        make_identity(nc, ident_f32[:])
 
         w1_dram = W1_words.rearrange("g p n t -> g p (n t)").bitcast(I32)
         w2_dram = W2_words.rearrange("g p n t -> g p (n t)").bitcast(I32)
@@ -77,29 +75,61 @@ def tile_node_interaction_w_kernel(
                 in_=dram[g0:g1, :, n0:n1].rearrange("g p n -> p g n"),
             )
 
-        nc.scalar.dma_start(out=bias_row[0:1, 0:H], in_=b1.rearrange("(o n) -> o n", o=1))
-        nc.scalar.dma_start(out=bias_row[0:1, H : H + D], in_=b2.rearrange("(o n) -> o n", o=1))
-        nc.sync.dma_start(out=x_rows[:, 0, :], in_=node_embed)
-        nc.sync.dma_start(out=x_rows[:, 1, :], in_=ori)
-        for quad in range(4):
-            nc.sync.dma_start(
-                out=w1_planes[32 * quad : 32 * quad + 16, :].bitcast(I32),
-                in_=s1_dram[:, 4 * quad : 4 * quad + 4, :],
-            )
-        for a in range(G2 // PLANES):
+        def load_scales1(n0, n1):
             for quad in range(4):
                 nc.sync.dma_start(
-                    out=w2_planes[32 * quad : 32 * quad + 16, a, :].bitcast(I32),
-                    in_=s2_dram[PLANES * a : PLANES * (a + 1), 4 * quad : 4 * quad + 4, :],
+                    out=w1_planes[32 * quad : 32 * quad + 16, n0:n1].bitcast(I32),
+                    in_=s1_dram[:, 4 * quad : 4 * quad + 4, n0 // PACK : n1 // PACK],
                 )
-        for pair in range(PAIRS):
+
+        def load_scales2():
+            for a in range(G2 // PLANES):
+                for quad in range(4):
+                    nc.sync.dma_start(
+                        out=w2_planes[32 * quad : 32 * quad + 16, a, :].bitcast(I32),
+                        in_=s2_dram[PLANES * a : PLANES * (a + 1), 4 * quad : 4 * quad + 4, :],
+                    )
+
+        def load_gate(n0, n1):
+            nc.sync.dma_start(out=gate[:, n0:n1], in_=x_edge_c[:, n0:n1])
+
+        def load_pair1(pair):
             for g in range(G1):
                 load_words(w1_words, w1_dram, g, g + 1, 2 * CHUNK * pair, 2 * CHUNK * (pair + 1))
-            if pair == 0:
-                nc.sync.dma_start(out=gate[:], in_=x_edge_c)
+
+        B1_ROWS = H // CHUNK
+        B2_ROWS = D // CHUNK
+        nc.scalar.dma_start(out=bias_rows[0:B1_ROWS, :], in_=b1.rearrange("(r n) -> r n", n=CHUNK))
+        nc.scalar.dma_start(out=bias_rows[B1_ROWS : B1_ROWS + B2_ROWS, :], in_=b2.rearrange("(r n) -> r n", n=CHUNK))
+        nc.sync.dma_start(out=x_rows[:, 0, :], in_=node_embed)
+        nc.sync.dma_start(out=x_rows[:, 1, :], in_=ori)
+        load_scales1(0, 2 * CHUNK)
+        load_pair1(0)
+        load_gate(0, H // 2)
+        load_scales1(2 * CHUNK, H)
+        load_pair1(1)
+        load_gate(H // 2, H)
+        load_pair1(2)
+        load_pair1(3)
+        load_scales2()
         for first, chunks, width, k_cut in BLOCKS:
             for g0 in range(0, G2, k_cut):
                 load_words(w2_words, w2_dram, g0, g0 + k_cut, first, first + chunks * width)
+
+        def spread_bias(k):
+            spread = psum.tile([P, 2 * CHUNK], BF16, tag="side", name="spread_%d" % k)
+            for j in range(2):
+                nc.tensor.matmul(
+                    out=spread[:, CHUNK * j : CHUNK * (j + 1)],
+                    lhsT=ident_bf16[:, 2 * k + j : 2 * k + j + 1].to_broadcast([P, P]),
+                    rhs=bias_rows[:],
+                    start=True,
+                    stop=True,
+                )
+            nc.scalar.copy(out=bias_all[:, 2 * CHUNK * k : 2 * CHUNK * (k + 1)], in_=spread[:])
+
+        spread_bias(0)
+        spread_bias(1)
 
         def quantise_x(g):
             nc.vector.quantize_mx(
@@ -122,18 +152,6 @@ def tile_node_interaction_w_kernel(
             if g >= 1:
                 quantise_x(g - 1)
         quantise_x(G1 - 1)
-
-        for k in range((H + D) // (2 * CHUNK)):
-            spread = psum.tile([P, 2 * CHUNK], BF16, tag="side", name="spread_%d" % k)
-            for j in range(2):
-                nc.tensor.matmul(
-                    out=spread[:, CHUNK * j : CHUNK * (j + 1)],
-                    lhsT=ones[:],
-                    rhs=bias_row[:, CHUNK * (2 * k + j) : CHUNK * (2 * k + j + 1)],
-                    start=True,
-                    stop=True,
-                )
-            nc.scalar.copy(out=bias_all[:, 2 * CHUNK * k : 2 * CHUNK * (k + 1)], in_=spread[:])
 
         sums1 = {}
         acts = {}
@@ -210,6 +228,9 @@ def tile_node_interaction_w_kernel(
                 quantise_h(pair - 2)
             if pair >= 1:
                 transpose_h(pair - 1)
+            if pair < 2:
+                spread_bias(2 + 2 * pair)
+                spread_bias(3 + 2 * pair)
             activate(pair)
         quantise_h(PAIRS - 2)
 

@@ -55,10 +55,13 @@ def tile_node_interaction_w_kernel(
         h_planes = keep.tile([P, G2, HALVES * E], U8, align_bytes=64)
         bias_rows = keep.tile([P, CHUNK], BF16, align_bytes=64)
         bias_all = keep.tile([P, H + D], BF16)
+        silu_seed = keep.tile([P, 8], F32)
         ident_f32 = keep.tile([P, P], F32)
         ident_bf16 = keep.tile([P, P], BF16)
 
         nc.vector.memset(bias_rows[:].bitcast(I32), 0)
+        nc.vector.memset(silu_seed[:], 0.0)
+        nc.scalar.activation(out=silu_seed[:], in_=silu_seed[:], func=SILU)
         nc.vector.memset(w1_planes[:].bitcast(I32), 0)
         nc.vector.memset(w2_planes[:].rearrange("p a n -> p (a n)").bitcast(I32), 0)
         make_identity(nc, ident_bf16[:])
@@ -99,9 +102,9 @@ def tile_node_interaction_w_kernel(
 
         B1_ROWS = H // CHUNK
         B2_ROWS = D // CHUNK
-        nc.scalar.dma_start(out=bias_rows[0:B1_ROWS, :], in_=b1.rearrange("(r n) -> r n", n=CHUNK))
-        nc.scalar.dma_start(out=bias_rows[B1_ROWS : B1_ROWS + B2_ROWS, :], in_=b2.rearrange("(r n) -> r n", n=CHUNK))
         nc.sync.dma_start(out=x_rows[:, 0, :], in_=node_embed)
+        nc.sync.dma_start(out=bias_rows[0:B1_ROWS, :], in_=b1.rearrange("(r n) -> r n", n=CHUNK))
+        nc.sync.dma_start(out=bias_rows[B1_ROWS : B1_ROWS + B2_ROWS, :], in_=b2.rearrange("(r n) -> r n", n=CHUNK))
         nc.sync.dma_start(out=x_rows[:, 1, :], in_=ori)
         load_scales1(0, 2 * CHUNK)
         load_pair1(0)
@@ -116,6 +119,8 @@ def tile_node_interaction_w_kernel(
             for g0 in range(0, G2, k_cut):
                 load_words(w2_words, w2_dram, g0, g0 + k_cut, first, first + chunks * width)
 
+        spreads = {}
+
         def spread_bias(k):
             spread = psum.tile([P, 2 * CHUNK], BF16, tag="side", name="spread_%d" % k)
             for j in range(2):
@@ -126,10 +131,10 @@ def tile_node_interaction_w_kernel(
                     start=True,
                     stop=True,
                 )
-            nc.scalar.copy(out=bias_all[:, 2 * CHUNK * k : 2 * CHUNK * (k + 1)], in_=spread[:])
+            spreads[k] = spread
 
-        spread_bias(0)
-        spread_bias(1)
+        def keep_bias(k):
+            nc.scalar.copy(out=bias_all[:, 2 * CHUNK * k : 2 * CHUNK * (k + 1)], in_=spreads[k][:])
 
         def quantise_x(g):
             nc.vector.quantize_mx(
@@ -138,16 +143,25 @@ def tile_node_interaction_w_kernel(
                 in_=x_grouped[:, g].rearrange("p h r t -> p (h r t)"),
             )
 
-        for g in range(G1):
-            x_t = psum.tile([P, HALVES, 2, E], F32, tag="acc", name="x_t_%d" % g)
-            for h in range(HALVES):
-                pairs_of_k = x_rows[:, h, :].bitcast(F32)
+        x_t = [psum.tile([P, HALVES, 2, E], F32, tag="acc", name="x_t_%d" % g) for g in range(G1)]
+
+        def transpose_x(h):
+            pairs_of_k = x_rows[:, h, :].bitcast(F32)
+            for g in range(G1):
                 for u in range(2):
                     nc.tensor.transpose(
-                        x_t[:, h, u, :], pairs_of_k[:, 256 * g + u : 256 * (g + 1) : 2], ident_f32[:]
+                        x_t[g][:, h, u, :], pairs_of_k[:, 256 * g + u : 256 * (g + 1) : 2], ident_f32[:]
                     )
+
+        transpose_x(0)
+        spread_bias(0)
+        keep_bias(0)
+        transpose_x(1)
+        spread_bias(1)
+        keep_bias(1)
+        for g in range(G1):
             nc.vector.tensor_copy(
-                out=x_grouped[:, g].bitcast(F32), in_=x_t[:].rearrange("p h u r -> p h r u")
+                out=x_grouped[:, g].bitcast(F32), in_=x_t[g][:].rearrange("p h u r -> p h r u")
             )
             if g >= 1:
                 quantise_x(g - 1)
@@ -159,16 +173,16 @@ def tile_node_interaction_w_kernel(
         h_t = {}
         h_grouped = {}
 
-        def by_t(columns):
-            return columns.rearrange("p (q t) -> p t q", t=PACK)
+        def by_pair(columns):
+            return columns.rearrange("p (q u e) -> p u q e", u=2, e=2)
 
         def passes1(pair):
             chunks = (2 * pair, 2 * pair + 1)
             for c in chunks:
                 for h in range(HALVES):
                     sums1[(c, h)] = psum.tile([P, CHUNK], F32, tag="acc", name="sums1_%d_%d" % (c, h))
-                acts[c] = work.tile([P, HALVES, PACK, E], F32, tag="acts", bufs=4, name="acts_%d" % c)
-                h_sorted[c] = work.tile([P, HALVES, PACK, E], BF16, tag="h_sorted", bufs=4, name="h_sorted_%d" % c)
+                acts[c] = work.tile([P, HALVES, 2, E, 2], F32, tag="acts", bufs=4, name="acts_%d" % c)
+                h_sorted[c] = work.tile([P, HALVES, 2, E, 2], BF16, tag="h_sorted", bufs=4, name="h_sorted_%d" % c)
             for g in range(G1):
                 for c in chunks:
                     for h in range(HALVES):
@@ -188,33 +202,35 @@ def tile_node_interaction_w_kernel(
                 for h in range(HALVES):
                     nc.vector.tensor_tensor(
                         out=acts[c][:, h],
-                        in0=by_t(sums1[(c, h)][:]),
-                        in1=by_t(bias_all[:, CHUNK * c : CHUNK * (c + 1)]),
+                        in0=by_pair(sums1[(c, h)][:]),
+                        in1=by_pair(bias_all[:, CHUNK * c : CHUNK * (c + 1)]),
                         op=ADD,
                     )
             for c in chunks:
                 for h in range(HALVES):
                     nc.scalar.activation(out=acts[c][:, h], in_=acts[c][:, h], func=SILU)
             for c in chunks:
-                nc.vector.tensor_tensor(
-                    out=h_sorted[c][:],
-                    in0=acts[c][:],
-                    in1=by_t(gate[:, CHUNK * c : CHUNK * (c + 1)]).unsqueeze(1).to_broadcast([P, HALVES, PACK, E]),
-                    op=MULT,
-                )
+                for h in range(HALVES):
+                    nc.vector.tensor_tensor(
+                        out=h_sorted[c][:, h],
+                        in0=acts[c][:, h],
+                        in1=by_pair(gate[:, CHUNK * c : CHUNK * (c + 1)]),
+                        op=MULT,
+                    )
 
         def transpose_h(pair):
             for c in (2 * pair, 2 * pair + 1):
-                h_t[c] = psum.tile([P, HALVES, PACK, E], BF16, tag="side", name="h_t_%d" % c)
+                h_t[c] = psum.tile([P, HALVES, 2, E], F32, tag="side", name="h_t_%d" % c)
                 for h in range(HALVES):
-                    for t in range(PACK):
-                        nc.tensor.transpose(h_t[c][:, h, t, :], h_sorted[c][:, h, t, :], ident_bf16[:])
+                    for u in range(2):
+                        pairs_of_k = h_sorted[c][:, h, u].rearrange("p q e -> p (q e)").bitcast(F32)
+                        nc.tensor.transpose(h_t[c][:, h, u, :], pairs_of_k, ident_f32[:])
 
         def quantise_h(pair):
             chunks = (2 * pair, 2 * pair + 1)
             for c in chunks:
                 h_grouped[c] = work.tile([P, HALVES, E, PACK], BF16, tag="h_grouped", name="h_grouped_%d" % c, align_bytes=64)
-                nc.scalar.copy(out=h_grouped[c][:], in_=h_t[c][:].rearrange("p h t r -> p h r t"))
+                nc.scalar.copy(out=h_grouped[c][:].bitcast(F32), in_=h_t[c][:].rearrange("p h u r -> p h r u"))
             for c in chunks:
                 nc.vector.quantize_mx(
                     out=h_words[:, c, :].bitcast(FP8X4),
@@ -232,6 +248,9 @@ def tile_node_interaction_w_kernel(
                 spread_bias(2 + 2 * pair)
                 spread_bias(3 + 2 * pair)
             activate(pair)
+            if pair < 2:
+                keep_bias(2 + 2 * pair)
+                keep_bias(3 + 2 * pair)
         quantise_h(PAIRS - 2)
 
         out_rows = out.rearrange("e a c -> e (a c)")

@@ -28,6 +28,8 @@ PLANES = 4
 
 BLOCKS = ((0, 2, 512, 2), (1024, 1, 512, 4), (1536, 1, 256, 8), (1792, 1, 256, 4))
 
+WARM = 4
+
 FLOPS = 2 * (HALVES * E) * D * H * 2
 
 
@@ -54,12 +56,13 @@ def tile_node_interaction_w_kernel(
         h_words = keep.tile([P, G2, HALVES * E], U32, align_bytes=64)
         h_planes = keep.tile([P, G2, HALVES * E], U8, align_bytes=64)
         bias_rows = keep.tile([P, CHUNK], BF16, align_bytes=64)
+        idle = keep.tile([P, CHUNK], BF16, align_bytes=64)
         bias_all = keep.tile([P, H + D], BF16)
         silu_seed = keep.tile([P, 8], F32)
         ident_f32 = keep.tile([P, P], F32)
         ident_bf16 = keep.tile([P, P], BF16)
 
-        nc.vector.memset(bias_rows[:].bitcast(I32), 0)
+        nc.vector.memset(idle[:].bitcast(I32), 0)
         nc.vector.memset(silu_seed[:], 0.0)
         nc.scalar.activation(out=silu_seed[:], in_=silu_seed[:], func=SILU)
         nc.vector.memset(w1_planes[:].bitcast(I32), 0)
@@ -100,11 +103,18 @@ def tile_node_interaction_w_kernel(
             for g in range(G1):
                 load_words(w1_words, w1_dram, g, g + 1, 2 * CHUNK * pair, 2 * CHUNK * (pair + 1))
 
-        B1_ROWS = H // CHUNK
-        B2_ROWS = D // CHUNK
+        def load_bias(p0, b):
+            rows = b.rearrange("(r n) -> r n", n=CHUNK)
+            count = rows.shape[0]
+            copies = P // 2 // count
+            nc.sync.dma_start(
+                out=bias_rows[p0 : p0 + P // 2, :],
+                in_=rows.unsqueeze(0).to_broadcast([copies, count, CHUNK]),
+            )
+
+        load_bias(0, b1)
+        load_bias(P // 2, b2)
         nc.sync.dma_start(out=x_rows[:, 0, :], in_=node_embed)
-        nc.sync.dma_start(out=bias_rows[0:B1_ROWS, :], in_=b1.rearrange("(r n) -> r n", n=CHUNK))
-        nc.sync.dma_start(out=bias_rows[B1_ROWS : B1_ROWS + B2_ROWS, :], in_=b2.rearrange("(r n) -> r n", n=CHUNK))
         nc.sync.dma_start(out=x_rows[:, 1, :], in_=ori)
         load_scales1(0, 2 * CHUNK)
         load_pair1(0)
@@ -121,12 +131,16 @@ def tile_node_interaction_w_kernel(
 
         spreads = {}
 
+        def bias_row(k, j):
+            run = 2 * k + j
+            return run if run < H // CHUNK else P // 2 + run - H // CHUNK
+
         def spread_bias(k):
             spread = psum.tile([P, 2 * CHUNK], BF16, tag="side", name="spread_%d" % k)
             for j in range(2):
                 nc.tensor.matmul(
                     out=spread[:, CHUNK * j : CHUNK * (j + 1)],
-                    lhsT=ident_bf16[:, 2 * k + j : 2 * k + j + 1].to_broadcast([P, P]),
+                    lhsT=ident_bf16[:, bias_row(k, j) : bias_row(k, j) + 1].to_broadcast([P, P]),
                     rhs=bias_rows[:],
                     start=True,
                     stop=True,
@@ -153,12 +167,18 @@ def tile_node_interaction_w_kernel(
                         x_t[g][:, h, u, :], pairs_of_k[:, 256 * g + u : 256 * (g + 1) : 2], ident_f32[:]
                     )
 
+        warm = psum.tile([P, CHUNK], F32, tag="side", name="warm")
+        for k in range(WARM):
+            nc.tensor.matmul(out=warm[:], lhsT=idle[:, 0:P], rhs=idle[:], start=True, stop=True)
+        def biases(k0, k1):
+            for k in range(k0, k1):
+                spread_bias(k)
+                keep_bias(k)
+
+        biases(0, 2)
         transpose_x(0)
-        spread_bias(0)
-        keep_bias(0)
         transpose_x(1)
-        spread_bias(1)
-        keep_bias(1)
+        biases(2, 4)
         for g in range(G1):
             nc.vector.tensor_copy(
                 out=x_grouped[:, g].bitcast(F32), in_=x_t[g][:].rearrange("p h u r -> p h r u")
@@ -244,13 +264,9 @@ def tile_node_interaction_w_kernel(
                 quantise_h(pair - 2)
             if pair >= 1:
                 transpose_h(pair - 1)
-            if pair < 2:
-                spread_bias(2 + 2 * pair)
-                spread_bias(3 + 2 * pair)
             activate(pair)
-            if pair < 2:
-                keep_bias(2 + 2 * pair)
-                keep_bias(3 + 2 * pair)
+            if pair == 0:
+                biases(4, 6)
         quantise_h(PAIRS - 2)
 
         out_rows = out.rearrange("e a c -> e (a c)")
@@ -296,7 +312,7 @@ def tile_node_interaction_w_kernel(
             sums = open2(block, ring)
             for g0 in range(0, G2, k_cut):
                 passes2(sums, width, g0, g0 + k_cut)
-                if first == 0 and g0 == 0:
+                if first == 0 and g0 == 2:
                     transpose_h(PAIRS - 1)
                     quantise_h(PAIRS - 1)
             if before is not None:

@@ -63,6 +63,7 @@ def tile_node_interaction_w_kernel(
         ident_bf16 = keep.tile([P, P], BF16)
 
         nc.vector.memset(idle[:].bitcast(I32), 0)
+        nc.vector.memset(bias_rows[:].bitcast(I32), 0)
         nc.vector.memset(silu_seed[:], 0.0)
         nc.scalar.activation(out=silu_seed[:], in_=silu_seed[:], func=SILU)
         nc.vector.memset(w1_planes[:].bitcast(I32), 0)
@@ -103,19 +104,12 @@ def tile_node_interaction_w_kernel(
             for g in range(G1):
                 load_words(w1_words, w1_dram, g, g + 1, 2 * CHUNK * pair, 2 * CHUNK * (pair + 1))
 
-        def load_bias(p0, b):
-            rows = b.rearrange("(r n) -> r n", n=CHUNK)
-            count = rows.shape[0]
-            copies = P // 2 // count
-            nc.sync.dma_start(
-                out=bias_rows[p0 : p0 + P // 2, :],
-                in_=rows.unsqueeze(0).to_broadcast([copies, count, CHUNK]),
-            )
-
-        load_bias(0, b1)
-        load_bias(P // 2, b2)
+        B1_ROWS = H // CHUNK
+        B2_ROWS = D // CHUNK
         nc.sync.dma_start(out=x_rows[:, 0, :], in_=node_embed)
         nc.sync.dma_start(out=x_rows[:, 1, :], in_=ori)
+        nc.sync.dma_start(out=bias_rows[0:B1_ROWS, :], in_=b1.rearrange("(r n) -> r n", n=CHUNK))
+        nc.sync.dma_start(out=bias_rows[B1_ROWS : B1_ROWS + B2_ROWS, :], in_=b2.rearrange("(r n) -> r n", n=CHUNK))
         load_scales1(0, 2 * CHUNK)
         load_pair1(0)
         load_gate(0, H // 2)
@@ -131,16 +125,12 @@ def tile_node_interaction_w_kernel(
 
         spreads = {}
 
-        def bias_row(k, j):
-            run = 2 * k + j
-            return run if run < H // CHUNK else P // 2 + run - H // CHUNK
-
         def spread_bias(k):
             spread = psum.tile([P, 2 * CHUNK], BF16, tag="side", name="spread_%d" % k)
             for j in range(2):
                 nc.tensor.matmul(
                     out=spread[:, CHUNK * j : CHUNK * (j + 1)],
-                    lhsT=ident_bf16[:, bias_row(k, j) : bias_row(k, j) + 1].to_broadcast([P, P]),
+                    lhsT=ident_bf16[:, 2 * k + j : 2 * k + j + 1].to_broadcast([P, P]),
                     rhs=bias_rows[:],
                     start=True,
                     stop=True,
@@ -175,10 +165,9 @@ def tile_node_interaction_w_kernel(
                 spread_bias(k)
                 keep_bias(k)
 
-        biases(0, 2)
         transpose_x(0)
         transpose_x(1)
-        biases(2, 4)
+        biases(0, 2)
         for g in range(G1):
             nc.vector.tensor_copy(
                 out=x_grouped[:, g].bitcast(F32), in_=x_t[g][:].rearrange("p h u r -> p h r u")
@@ -265,8 +254,8 @@ def tile_node_interaction_w_kernel(
             if pair >= 1:
                 transpose_h(pair - 1)
             activate(pair)
-            if pair == 0:
-                biases(4, 6)
+            if pair < 2:
+                biases(2 + 2 * pair, 4 + 2 * pair)
         quantise_h(PAIRS - 2)
 
         out_rows = out.rearrange("e a c -> e (a c)")

@@ -26,8 +26,6 @@ CHUNK = 512
 PAIRS = H // (2 * CHUNK)
 PLANES = 4
 
-BLOCKS = ((0, 2, 512, 2), (1024, 1, 512, 4), (1536, 1, 256, 8), (1792, 1, 256, 4))
-
 WARM = 4
 
 FLOPS = 2 * (HALVES * E) * D * H * 2
@@ -89,13 +87,12 @@ def tile_node_interaction_w_kernel(
                     in_=s1_dram[:, 4 * quad : 4 * quad + 4, n0 // PACK : n1 // PACK],
                 )
 
-        def load_scales2():
-            for a in range(G2 // PLANES):
-                for quad in range(4):
-                    nc.sync.dma_start(
-                        out=w2_planes[32 * quad : 32 * quad + 16, a, :].bitcast(I32),
-                        in_=s2_dram[PLANES * a : PLANES * (a + 1), 4 * quad : 4 * quad + 4, :],
-                    )
+        def load_scales2(a):
+            for quad in range(4):
+                nc.sync.dma_start(
+                    out=w2_planes[32 * quad : 32 * quad + 16, a, :].bitcast(I32),
+                    in_=s2_dram[PLANES * a : PLANES * (a + 1), 4 * quad : 4 * quad + 4, :],
+                )
 
         def load_gate(n0, n1):
             nc.sync.dma_start(out=gate[:, n0:n1], in_=x_edge_c[:, n0:n1])
@@ -118,10 +115,20 @@ def tile_node_interaction_w_kernel(
         load_gate(H // 2, H)
         load_pair1(2)
         load_pair1(3)
-        load_scales2()
-        for first, chunks, width, k_cut in BLOCKS:
-            for g0 in range(0, G2, k_cut):
-                load_words(w2_words, w2_dram, g0, g0 + k_cut, first, first + chunks * width)
+        def load2(g0, g1, n0, n1):
+            load_words(w2_words, w2_dram, g0, g1, n0, n1)
+
+        for a in range(G2 // PLANES):
+            load_scales2(a)
+            for g in range(PLANES * a, PLANES * (a + 1)):
+                load2(g, g + 1, 0, D // 2)
+        for g in range(G2 // 2):
+            load2(g, g + 1, D // 2, D)
+        for g in (4, 6):
+            load2(g, g + 2, 2 * CHUNK, 3 * CHUNK)
+        load2(4, 8, 3 * CHUNK, 3 * CHUNK + CHUNK // 2)
+        for g in (4, 6):
+            load2(g, g + 2, 3 * CHUNK + CHUNK // 2, D)
 
         spreads = {}
 
@@ -260,16 +267,12 @@ def tile_node_interaction_w_kernel(
 
         out_rows = out.rearrange("e a c -> e (a c)")
 
-        def open2(block, ring):
-            first, chunks, width, k_cut = block
-            return [
-                (psum.tile([P, width], F32, tag=ring, name="sums2_%d_%d" % (first + width * j, h)), h, first + width * j)
-                for j in range(chunks)
-                for h in range(HALVES)
-            ]
+        def open2(n0, width, ring):
+            return [(psum.tile([P, width], F32, tag=ring, name="sums2_%d_%d" % (n0, h)), h, n0) for h in range(HALVES)]
 
-        def passes2(sums, width, g0, g1):
+        def passes2(sums, g0, g1):
             for acc, h, n0 in sums:
+                width = acc.shape[1]
                 for g in range(g0, g1):
                     nc.tensor.matmul_mx(
                         out=acc[:],
@@ -281,30 +284,36 @@ def tile_node_interaction_w_kernel(
                         stop=(g == G2 - 1),
                     )
 
-        def finish2(sums, width):
-            for j in range(len(sums) // HALVES):
-                n0 = sums[HALVES * j][2]
-                y = work.tile([P, HALVES, CHUNK], F32, tag="acts", bufs=4, name="y_%d" % n0)
-                for acc, h, n0_same in sums[HALVES * j : HALVES * (j + 1)]:
-                    nc.vector.tensor_tensor(
-                        out=y[:, h, 0:width], in0=acc[:], in1=bias_all[:, H + n0 : H + n0 + width], op=ADD
-                    )
-                    nc.scalar.activation(out=y[:, h, 0:width], in_=y[:, h, 0:width], func=SILU)
-                both = work.tile([P, CHUNK], F32, tag="both", name="both_%d" % n0)
-                nc.vector.tensor_tensor(out=both[:, 0:width], in0=y[:, 0, 0:width], in1=y[:, 1, 0:width], op=ADD)
-                nc.sync.dma_start(out=out_rows[:, n0 : n0 + width], in_=both[:, 0:width])
+        def finish2(sums):
+            n0 = sums[0][2]
+            width = sums[0][0].shape[1]
+            y = work.tile([P, HALVES, CHUNK], F32, tag="acts", bufs=4, name="y_%d" % n0)
+            for acc, h, n0_same in sums:
+                nc.vector.tensor_tensor(
+                    out=y[:, h, 0:width], in0=acc[:], in1=bias_all[:, H + n0 : H + n0 + width], op=ADD
+                )
+                nc.scalar.activation(out=y[:, h, 0:width], in_=y[:, h, 0:width], func=SILU)
+            both = work.tile([P, CHUNK], F32, tag="both", name="both_%d" % n0)
+            nc.vector.tensor_tensor(out=both[:, 0:width], in0=y[:, 0, 0:width], in1=y[:, 1, 0:width], op=ADD)
+            nc.sync.dma_start(out=out_rows[:, n0 : n0 + width], in_=both[:, 0:width])
 
-        rings = ("acc", "side", "side", "acc")
-        before = None
-        for block, ring in zip(BLOCKS, rings):
-            first, chunks, width, k_cut = block
-            sums = open2(block, ring)
-            for g0 in range(0, G2, k_cut):
-                passes2(sums, width, g0, g0 + k_cut)
-                if first == 0 and g0 == 2:
-                    transpose_h(PAIRS - 1)
-                    quantise_h(PAIRS - 1)
-            if before is not None:
-                finish2(before[0], before[1])
-            before = (sums, width)
-        finish2(before[0], before[1])
+        left = [open2(n0, CHUNK, "acc") for n0 in (0, CHUNK)]
+        for g in range(G2):
+            for sums in left:
+                passes2(sums, g, g + 1)
+            if g == 3:
+                transpose_h(PAIRS - 1)
+                quantise_h(PAIRS - 1)
+        for sums in left:
+            finish2(sums)
+        third = open2(2 * CHUNK, CHUNK, "side")
+        halves = [open2(3 * CHUNK, CHUNK // 2, "side"), open2(3 * CHUNK + CHUNK // 2, CHUNK // 2, "acc")]
+        for g in range(G2 // 2):
+            for sums in [third] + halves:
+                passes2(sums, g, g + 1)
+        for g0 in (4, 6):
+            passes2(third, g0, g0 + 2)
+        finish2(third)
+        for sums in halves:
+            passes2(sums, 4, 8)
+            finish2(sums)

@@ -284,15 +284,22 @@ def tile_node_interaction_w_kernel(
                         stop=(g == G2 - 1),
                     )
 
-        def finish2(sums):
+        ys = {}
+
+        def activate2(sums):
             n0 = sums[0][2]
             width = sums[0][0].shape[1]
-            y = work.tile([P, HALVES, CHUNK], F32, tag="acts", bufs=4, name="y_%d" % n0)
+            ys[n0] = y = work.tile([P, HALVES, CHUNK], F32, tag="acts", bufs=4, name="y_%d" % n0)
             for acc, h, n0_same in sums:
                 nc.vector.tensor_tensor(
                     out=y[:, h, 0:width], in0=acc[:], in1=bias_all[:, H + n0 : H + n0 + width], op=ADD
                 )
                 nc.scalar.activation(out=y[:, h, 0:width], in_=y[:, h, 0:width], func=SILU)
+
+        def finish2(sums):
+            n0 = sums[0][2]
+            width = sums[0][0].shape[1]
+            y = ys[n0]
             both = work.tile([P, CHUNK], F32, tag="both", name="both_%d" % n0)
             nc.vector.tensor_tensor(out=both[:, 0:width], in0=y[:, 0, 0:width], in1=y[:, 1, 0:width], op=ADD)
             nc.sync.dma_start(out=out_rows[:, n0 : n0 + width], in_=both[:, 0:width])
@@ -305,6 +312,8 @@ def tile_node_interaction_w_kernel(
                 transpose_h(PAIRS - 1)
                 quantise_h(PAIRS - 1)
         for sums in left:
+            activate2(sums)
+        for sums in left:
             finish2(sums)
         third = open2(2 * CHUNK, CHUNK, "side")
         halves = [open2(3 * CHUNK, CHUNK // 2, "side"), open2(3 * CHUNK + CHUNK // 2, CHUNK // 2, "acc")]
@@ -313,7 +322,12 @@ def tile_node_interaction_w_kernel(
                 passes2(sums, g, g + 1)
         for g0 in (4, 6):
             passes2(third, g0, g0 + 2)
+        activate2(third)
+        passes2(halves[0], 4, 8)
+        activate2(halves[0])
         finish2(third)
+        for g0 in (4, 6):
+            passes2(halves[1], g0, g0 + 2)
+        activate2(halves[1])
         for sums in halves:
-            passes2(sums, 4, 8)
             finish2(sums)

@@ -300,7 +300,7 @@ def tile_node_interaction_w_kernel(
             n0 = sums[0][2]
             width = sums[0][0].shape[1]
             y = ys[n0]
-            both = work.tile([P, CHUNK], F32, tag="both", name="both_%d" % n0)
+            both = work.tile([P, CHUNK], F32, tag="both", bufs=5, name="both_%d" % n0)
             nc.vector.tensor_tensor(out=both[:, 0:width], in0=y[:, 0, 0:width], in1=y[:, 1, 0:width], op=ADD)
             nc.sync.dma_start(out=out_rows[:, n0 : n0 + width], in_=both[:, 0:width])
 

@@ -26,6 +26,8 @@ CHUNK = 512
 PAIRS = H // (2 * CHUNK)
 PLANES = 4
 
+LEFT = 3 * CHUNK
+
 WARM = 4
 
 FLOPS = 2 * (HALVES * E) * D * H * 2
@@ -40,7 +42,10 @@ def tile_node_interaction_w_kernel(
         ctx.enter_context(tc.manual_schedule())
         keep = ctx.enter_context(tc.tile_pool(name="keep", bufs=1))
         work = ctx.enter_context(tc.tile_pool(name="work", bufs=2))
-        psum = ctx.enter_context(tc.psum_pool(name="psum", bufs=4))
+        psum = ctx.enter_context(tc.psum_pool(name="psum", bufs=1))
+
+        def ring(tag, shape, dtype, name):
+            return psum.tile(shape, dtype, tag=tag, bufs={"acc": 6, "side": 2}[tag], name=name)
 
         w1_words = keep.tile([P, G1, H], U32, align_bytes=64)
         w2_words = keep.tile([P, G2, D], U32, align_bytes=64)
@@ -80,11 +85,11 @@ def tile_node_interaction_w_kernel(
                 in_=dram[g0:g1, :, n0:n1].rearrange("g p n -> p g n"),
             )
 
-        def load_scales1(n0, n1):
+        def load_scales1():
             for quad in range(4):
                 nc.sync.dma_start(
-                    out=w1_planes[32 * quad : 32 * quad + 16, n0:n1].bitcast(I32),
-                    in_=s1_dram[:, 4 * quad : 4 * quad + 4, n0 // PACK : n1 // PACK],
+                    out=w1_planes[32 * quad : 32 * quad + 16, :].bitcast(I32),
+                    in_=s1_dram[:, 4 * quad : 4 * quad + 4, :],
                 )
 
         def load_scales2(a):
@@ -93,9 +98,6 @@ def tile_node_interaction_w_kernel(
                     out=w2_planes[32 * quad : 32 * quad + 16, a, :].bitcast(I32),
                     in_=s2_dram[PLANES * a : PLANES * (a + 1), 4 * quad : 4 * quad + 4, :],
                 )
-
-        def load_gate(n0, n1):
-            nc.sync.dma_start(out=gate[:, n0:n1], in_=x_edge_c[:, n0:n1])
 
         def load_pair1(pair):
             for g in range(G1):
@@ -107,33 +109,28 @@ def tile_node_interaction_w_kernel(
         nc.sync.dma_start(out=x_rows[:, 1, :], in_=ori)
         nc.sync.dma_start(out=bias_rows[0:B1_ROWS, :], in_=b1.rearrange("(r n) -> r n", n=CHUNK))
         nc.sync.dma_start(out=bias_rows[B1_ROWS : B1_ROWS + B2_ROWS, :], in_=b2.rearrange("(r n) -> r n", n=CHUNK))
-        load_scales1(0, 2 * CHUNK)
+        load_scales1()
         load_pair1(0)
-        load_gate(0, H // 2)
-        load_scales1(2 * CHUNK, H)
-        load_pair1(1)
-        load_gate(H // 2, H)
-        load_pair1(2)
-        load_pair1(3)
+        nc.sync.dma_start(out=gate[:], in_=x_edge_c)
+        for pair in range(1, PAIRS):
+            load_pair1(pair)
         def load2(g0, g1, n0, n1):
             load_words(w2_words, w2_dram, g0, g1, n0, n1)
 
         for a in range(G2 // PLANES):
             load_scales2(a)
             for g in range(PLANES * a, PLANES * (a + 1)):
-                load2(g, g + 1, 0, D // 2)
-        for g in range(G2 // 2):
-            load2(g, g + 1, D // 2, D)
-        for g in (4, 6):
-            load2(g, g + 2, 2 * CHUNK, 3 * CHUNK)
-        load2(4, 8, 3 * CHUNK, 3 * CHUNK + CHUNK // 2)
-        for g in (4, 6):
-            load2(g, g + 2, 3 * CHUNK + CHUNK // 2, D)
+                load2(g, g + 1, 0, LEFT)
+        for g in (0, 2):
+            load2(g, g + 2, LEFT, D)
+        load2(4, 6, LEFT, D)
+        for n0 in (LEFT, LEFT + CHUNK // 2):
+            load2(6, 8, n0, n0 + CHUNK // 2)
 
         spreads = {}
 
         def spread_bias(k):
-            spread = psum.tile([P, 2 * CHUNK], BF16, tag="side", name="spread_%d" % k)
+            spread = ring("acc" if k >= 4 else "side", [P, 2 * CHUNK], BF16, "spread_%d" % k)
             for j in range(2):
                 nc.tensor.matmul(
                     out=spread[:, CHUNK * j : CHUNK * (j + 1)],
@@ -154,7 +151,7 @@ def tile_node_interaction_w_kernel(
                 in_=x_grouped[:, g].rearrange("p h r t -> p (h r t)"),
             )
 
-        x_t = [psum.tile([P, HALVES, 2, E], F32, tag="acc", name="x_t_%d" % g) for g in range(G1)]
+        x_t = [ring("acc", [P, HALVES, 2, E], F32, "x_t_%d" % g) for g in range(G1)]
 
         def transpose_x(h):
             pairs_of_k = x_rows[:, h, :].bitcast(F32)
@@ -164,7 +161,7 @@ def tile_node_interaction_w_kernel(
                         x_t[g][:, h, u, :], pairs_of_k[:, 256 * g + u : 256 * (g + 1) : 2], ident_f32[:]
                     )
 
-        warm = psum.tile([P, CHUNK], F32, tag="side", name="warm")
+        warm = ring("side", [P, CHUNK], F32, "warm")
         for k in range(WARM):
             nc.tensor.matmul(out=warm[:], lhsT=idle[:, 0:P], rhs=idle[:], start=True, stop=True)
         def biases(k0, k1):
@@ -196,7 +193,7 @@ def tile_node_interaction_w_kernel(
             chunks = (2 * pair, 2 * pair + 1)
             for c in chunks:
                 for h in range(HALVES):
-                    sums1[(c, h)] = psum.tile([P, CHUNK], F32, tag="acc", name="sums1_%d_%d" % (c, h))
+                    sums1[(c, h)] = ring("acc", [P, CHUNK], F32, "sums1_%d_%d" % (c, h))
                 acts[c] = work.tile([P, HALVES, 2, E, 2], F32, tag="acts", bufs=4, name="acts_%d" % c)
                 h_sorted[c] = work.tile([P, HALVES, 2, E, 2], BF16, tag="h_sorted", bufs=4, name="h_sorted_%d" % c)
             for g in range(G1):
@@ -236,7 +233,7 @@ def tile_node_interaction_w_kernel(
 
         def transpose_h(pair):
             for c in (2 * pair, 2 * pair + 1):
-                h_t[c] = psum.tile([P, HALVES, 2, E], F32, tag="side", name="h_t_%d" % c)
+                h_t[c] = ring("side", [P, HALVES, 2, E], F32, "h_t_%d" % c)
                 for h in range(HALVES):
                     for u in range(2):
                         pairs_of_k = h_sorted[c][:, h, u].rearrange("p q e -> p (q e)").bitcast(F32)
@@ -261,14 +258,14 @@ def tile_node_interaction_w_kernel(
             if pair >= 1:
                 transpose_h(pair - 1)
             activate(pair)
-            if pair < 2:
-                biases(2 + 2 * pair, 4 + 2 * pair)
+            if pair == 0:
+                biases(2, 6)
         quantise_h(PAIRS - 2)
 
         out_rows = out.rearrange("e a c -> e (a c)")
 
-        def open2(n0, width, ring):
-            return [(psum.tile([P, width], F32, tag=ring, name="sums2_%d_%d" % (n0, h)), h, n0) for h in range(HALVES)]
+        def open2(n0, width, tag):
+            return [(ring(tag, [P, width], F32, "sums2_%d_%d" % (n0, h)), h, n0) for h in range(HALVES)]
 
         def passes2(sums, g0, g1):
             for acc, h, n0 in sums:
@@ -304,30 +301,25 @@ def tile_node_interaction_w_kernel(
             nc.vector.tensor_tensor(out=both[:, 0:width], in0=y[:, 0, 0:width], in1=y[:, 1, 0:width], op=ADD)
             nc.sync.dma_start(out=out_rows[:, n0 : n0 + width], in_=both[:, 0:width])
 
-        left = [open2(n0, CHUNK, "acc") for n0 in (0, CHUNK)]
+        left = [open2(n0, CHUNK, "acc") for n0 in range(0, LEFT, CHUNK)]
         for g in range(G2):
             for sums in left:
                 passes2(sums, g, g + 1)
-            if g == 3:
+            if g == 2:
                 transpose_h(PAIRS - 1)
                 quantise_h(PAIRS - 1)
         for sums in left:
             activate2(sums)
         for sums in left:
             finish2(sums)
-        third = open2(2 * CHUNK, CHUNK, "side")
-        halves = [open2(3 * CHUNK, CHUNK // 2, "side"), open2(3 * CHUNK + CHUNK // 2, CHUNK // 2, "acc")]
-        for g in range(G2 // 2):
-            for sums in [third] + halves:
-                passes2(sums, g, g + 1)
-        for g0 in (4, 6):
-            passes2(third, g0, g0 + 2)
-        activate2(third)
-        passes2(halves[0], 4, 8)
-        activate2(halves[0])
-        finish2(third)
-        for g0 in (4, 6):
-            passes2(halves[1], g0, g0 + 2)
-        activate2(halves[1])
+        halves = [open2(LEFT, CHUNK // 2, "side"), open2(LEFT + CHUNK // 2, CHUNK // 2, "acc")]
+        for g0 in (0, 2):
+            for sums in halves:
+                passes2(sums, g0, g0 + 2)
+        for sums in halves:
+            passes2(sums, 4, 6)
+        for sums in halves:
+            passes2(sums, 6, 8)
+            activate2(sums)
         for sums in halves:
             finish2(sums)

@@ -85,12 +85,15 @@ def tile_node_interaction_w_kernel(
                 in_=dram[g0:g1, :, n0:n1].rearrange("g p n -> p g n"),
             )
 
-        def load_scales1():
+        def load_scales1(n0, n1):
             for quad in range(4):
                 nc.sync.dma_start(
-                    out=w1_planes[32 * quad : 32 * quad + 16, :].bitcast(I32),
-                    in_=s1_dram[:, 4 * quad : 4 * quad + 4, :],
+                    out=w1_planes[32 * quad : 32 * quad + 16, n0:n1].bitcast(I32),
+                    in_=s1_dram[:, 4 * quad : 4 * quad + 4, n0 // PACK : n1 // PACK],
                 )
+
+        def load_gate(n0, n1):
+            nc.sync.dma_start(out=gate[:, n0:n1], in_=x_edge_c[:, n0:n1])
 
         def load_scales2(a):
             for quad in range(4):
@@ -109,11 +112,25 @@ def tile_node_interaction_w_kernel(
         nc.sync.dma_start(out=x_rows[:, 1, :], in_=ori)
         nc.sync.dma_start(out=bias_rows[0:B1_ROWS, :], in_=b1.rearrange("(r n) -> r n", n=CHUNK))
         nc.sync.dma_start(out=bias_rows[B1_ROWS : B1_ROWS + B2_ROWS, :], in_=b2.rearrange("(r n) -> r n", n=CHUNK))
-        load_scales1()
-        load_pair1(0)
-        nc.sync.dma_start(out=gate[:], in_=x_edge_c)
-        for pair in range(1, PAIRS):
-            load_pair1(pair)
+        load_scales1(0, 2048)
+        load_words(w1_words, w1_dram, 0, 0+1, 0, 1024)
+        load_words(w1_words, w1_dram, 1, 1+1, 0, 1024)
+        load_words(w1_words, w1_dram, 2, 2+1, 0, 1024)
+        load_words(w1_words, w1_dram, 3, 3+1, 0, 1024)
+        load_gate(0, 4096)
+        load_words(w1_words, w1_dram, 0, 0+1, 1024, 2048)
+        load_words(w1_words, w1_dram, 1, 1+1, 1024, 2048)
+        load_words(w1_words, w1_dram, 2, 2+1, 1024, 2048)
+        load_words(w1_words, w1_dram, 3, 3+1, 1024, 2048)
+        load_scales1(2048, 4096)
+        load_words(w1_words, w1_dram, 0, 0+1, 2048, 3072)
+        load_words(w1_words, w1_dram, 1, 1+1, 2048, 3072)
+        load_words(w1_words, w1_dram, 2, 2+1, 2048, 3072)
+        load_words(w1_words, w1_dram, 3, 3+1, 2048, 3072)
+        load_words(w1_words, w1_dram, 0, 0+1, 3072, 4096)
+        load_words(w1_words, w1_dram, 1, 1+1, 3072, 4096)
+        load_words(w1_words, w1_dram, 2, 2+1, 3072, 4096)
+        load_words(w1_words, w1_dram, 3, 3+1, 3072, 4096)
         def load2(g0, g1, n0, n1):
             load_words(w2_words, w2_dram, g0, g1, n0, n1)
 

@@ -76,8 +76,6 @@ def tile_node_interaction_w_kernel(
 
         w1_dram = W1_words.rearrange("g p n t -> g p (n t)").bitcast(I32)
         w2_dram = W2_words.rearrange("g p n t -> g p (n t)").bitcast(I32)
-        s1_dram = W1_scales.bitcast(I32)
-        s2_dram = W2_scales.bitcast(I32)
 
         def load_words(sbuf, dram, g0, g1, n0, n1):
             nc.sync.dma_start(
@@ -85,11 +83,11 @@ def tile_node_interaction_w_kernel(
                 in_=dram[g0:g1, :, n0:n1].rearrange("g p n -> p g n"),
             )
 
-        def load_scales1(n0, n1):
+        def load_scales1(queue, words, n0, n1):
             for quad in range(4):
-                nc.sync.dma_start(
-                    out=w1_planes[32 * quad : 32 * quad + 16, n0:n1].bitcast(I32),
-                    in_=s1_dram[:, 4 * quad : 4 * quad + 4, n0 // PACK : n1 // PACK],
+                queue.dma_start(
+                    out=w1_planes[32 * quad : 32 * quad + 16, n0:n1].bitcast(words),
+                    in_=W1_scales.bitcast(words)[:, 4 * quad : 4 * quad + 4, n0 // PACK : n1 // PACK],
                 )
 
         def load_gate(n0, n1):
@@ -97,9 +95,9 @@ def tile_node_interaction_w_kernel(
 
         def load_scales2(a):
             for quad in range(4):
-                nc.sync.dma_start(
-                    out=w2_planes[32 * quad : 32 * quad + 16, a, :].bitcast(I32),
-                    in_=s2_dram[PLANES * a : PLANES * (a + 1), 4 * quad : 4 * quad + 4, :],
+                nc.gpsimd.dma_start(
+                    out=w2_planes[32 * quad : 32 * quad + 16, a, :].bitcast(F32),
+                    in_=W2_scales.bitcast(F32)[PLANES * a : PLANES * (a + 1), 4 * quad : 4 * quad + 4, :],
                 )
 
         def load_pair1(pair):
@@ -112,7 +110,8 @@ def tile_node_interaction_w_kernel(
         nc.sync.dma_start(out=x_rows[:, 1, :], in_=ori)
         nc.sync.dma_start(out=bias_rows[0:B1_ROWS, :], in_=b1.rearrange("(r n) -> r n", n=CHUNK))
         nc.sync.dma_start(out=bias_rows[B1_ROWS : B1_ROWS + B2_ROWS, :], in_=b2.rearrange("(r n) -> r n", n=CHUNK))
-        load_scales1(0, 2048)
+        load_scales1(nc.sync, I32, 0, 2 * CHUNK)
+        load_scales1(nc.gpsimd, F32, 2 * CHUNK, H)
         load_words(w1_words, w1_dram, 0, 0+1, 0, 1024)
         load_words(w1_words, w1_dram, 1, 1+1, 0, 1024)
         load_words(w1_words, w1_dram, 2, 2+1, 0, 1024)
@@ -122,7 +121,8 @@ def tile_node_interaction_w_kernel(
         load_words(w1_words, w1_dram, 1, 1+1, 1024, 2048)
         load_words(w1_words, w1_dram, 2, 2+1, 1024, 2048)
         load_words(w1_words, w1_dram, 3, 3+1, 1024, 2048)
-        load_scales1(2048, 4096)
+        for a in range(G2 // PLANES):
+            load_scales2(a)
         load_words(w1_words, w1_dram, 0, 0+1, 2048, 3072)
         load_words(w1_words, w1_dram, 1, 1+1, 2048, 3072)
         load_words(w1_words, w1_dram, 2, 2+1, 2048, 3072)
@@ -135,7 +135,6 @@ def tile_node_interaction_w_kernel(
             load_words(w2_words, w2_dram, g0, g1, n0, n1)
 
         for a in range(G2 // PLANES):
-            load_scales2(a)
             for g in range(PLANES * a, PLANES * (a + 1)):
                 load2(g, g + 1, 0, LEFT)
         for g in (0, 2):

@@ -69,10 +69,9 @@ def tile_node_interaction_w_kernel(
         nc.vector.memset(bias_rows[:].bitcast(I32), 0)
         nc.vector.memset(silu_seed[:], 0.0)
         nc.scalar.activation(out=silu_seed[:], in_=silu_seed[:], func=SILU)
-        nc.vector.memset(w1_planes[:].bitcast(I32), 0)
-        nc.vector.memset(w2_planes[:].rearrange("p a n -> p (a n)").bitcast(I32), 0)
-        make_identity(nc, ident_bf16[:])
+        nc.vector.memset(w1_planes[:, 0 : 2 * CHUNK].bitcast(I32), 0)
         make_identity(nc, ident_f32[:])
+        make_identity(nc, ident_bf16[:])
 
         w1_dram = W1_words.rearrange("g p n t -> g p (n t)").bitcast(I32)
         w2_dram = W2_words.rearrange("g p n t -> g p (n t)").bitcast(I32)
@@ -106,31 +105,22 @@ def tile_node_interaction_w_kernel(
 
         B1_ROWS = H // CHUNK
         B2_ROWS = D // CHUNK
-        nc.sync.dma_start(out=x_rows[:, 0, :], in_=node_embed)
-        nc.sync.dma_start(out=x_rows[:, 1, :], in_=ori)
-        nc.sync.dma_start(out=bias_rows[0:B1_ROWS, :], in_=b1.rearrange("(r n) -> r n", n=CHUNK))
-        nc.sync.dma_start(out=bias_rows[B1_ROWS : B1_ROWS + B2_ROWS, :], in_=b2.rearrange("(r n) -> r n", n=CHUNK))
+        def load_bias(r0, rows, vector):
+            nc.gpsimd.dma_start(out=bias_rows[r0 : r0 + rows, :], in_=vector.rearrange("(r n) -> r n", n=CHUNK))
+
+        load_bias(0, B1_ROWS, b1)
+        load_bias(B1_ROWS, B2_ROWS, b2)
+        for k0 in (0, D // 2):
+            for h, rows in enumerate((node_embed, ori)):
+                nc.sync.dma_start(out=x_rows[:, h, k0 : k0 + D // 2], in_=rows[:, k0 : k0 + D // 2])
+        load_words(w1_words, w1_dram, 0, 1, 0, 2 * CHUNK)
         load_scales1(nc.sync, I32, 0, 2 * CHUNK)
-        load_scales1(nc.gpsimd, F32, 2 * CHUNK, H)
-        load_words(w1_words, w1_dram, 0, 0+1, 0, 1024)
-        load_words(w1_words, w1_dram, 1, 1+1, 0, 1024)
-        load_words(w1_words, w1_dram, 2, 2+1, 0, 1024)
-        load_words(w1_words, w1_dram, 3, 3+1, 0, 1024)
-        load_gate(0, 4096)
-        load_words(w1_words, w1_dram, 0, 0+1, 1024, 2048)
-        load_words(w1_words, w1_dram, 1, 1+1, 1024, 2048)
-        load_words(w1_words, w1_dram, 2, 2+1, 1024, 2048)
-        load_words(w1_words, w1_dram, 3, 3+1, 1024, 2048)
-        for a in range(G2 // PLANES):
-            load_scales2(a)
-        load_words(w1_words, w1_dram, 0, 0+1, 2048, 3072)
-        load_words(w1_words, w1_dram, 1, 1+1, 2048, 3072)
-        load_words(w1_words, w1_dram, 2, 2+1, 2048, 3072)
-        load_words(w1_words, w1_dram, 3, 3+1, 2048, 3072)
-        load_words(w1_words, w1_dram, 0, 0+1, 3072, 4096)
-        load_words(w1_words, w1_dram, 1, 1+1, 3072, 4096)
-        load_words(w1_words, w1_dram, 2, 2+1, 3072, 4096)
-        load_words(w1_words, w1_dram, 3, 3+1, 3072, 4096)
+        for g in range(1, G1):
+            load_words(w1_words, w1_dram, g, g + 1, 0, 2 * CHUNK)
+        for pair in range(1, PAIRS):
+            load_gate(2 * CHUNK * (pair - 1), 2 * CHUNK * pair)
+            load_pair1(pair)
+        load_gate(H - 2 * CHUNK, H)
         def load2(g0, g1, n0, n1):
             load_words(w2_words, w2_dram, g0, g1, n0, n1)
 
@@ -169,9 +159,9 @@ def tile_node_interaction_w_kernel(
 
         x_t = [ring("acc", [P, HALVES, 2, E], F32, "x_t_%d" % g) for g in range(G1)]
 
-        def transpose_x(h):
-            pairs_of_k = x_rows[:, h, :].bitcast(F32)
-            for g in range(G1):
+        def transpose_x(g):
+            for h in range(HALVES):
+                pairs_of_k = x_rows[:, h, :].bitcast(F32)
                 for u in range(2):
                     nc.tensor.transpose(
                         x_t[g][:, h, u, :], pairs_of_k[:, 256 * g + u : 256 * (g + 1) : 2], ident_f32[:]
@@ -185,16 +175,17 @@ def tile_node_interaction_w_kernel(
                 spread_bias(k)
                 keep_bias(k)
 
-        transpose_x(0)
-        transpose_x(1)
-        biases(0, 2)
         for g in range(G1):
-            nc.vector.tensor_copy(
-                out=x_grouped[:, g].bitcast(F32), in_=x_t[g][:].rearrange("p h u r -> p h r u")
-            )
-            if g >= 1:
+            transpose_x(g)
+            copy = nc.vector.tensor_copy if g % 2 == 0 else nc.scalar.copy
+            copy(out=x_grouped[:, g].bitcast(F32), in_=x_t[g][:].rearrange("p h u r -> p h r u"))
+            if g % 2 == 1:
                 quantise_x(g - 1)
-        quantise_x(G1 - 1)
+                quantise_x(g)
+            if g == 1:
+                nc.vector.memset(w1_planes[:, 2 * CHUNK : H].bitcast(I32), 0)
+                load_scales1(nc.gpsimd, F32, 2 * CHUNK, H)
+        biases(0, 2)
 
         sums1 = {}
         acts = {}
@@ -276,6 +267,9 @@ def tile_node_interaction_w_kernel(
             activate(pair)
             if pair == 0:
                 biases(2, 6)
+                nc.vector.memset(w2_planes[:].rearrange("p a n -> p (a n)").bitcast(I32), 0)
+                for a in range(G2 // PLANES):
+                    load_scales2(a)
         quantise_h(PAIRS - 2)
 
         out_rows = out.rearrange("e a c -> e (a c)")
@@ -318,24 +312,18 @@ def tile_node_interaction_w_kernel(
             nc.sync.dma_start(out=out_rows[:, n0 : n0 + width], in_=both[:, 0:width])
 
         left = [open2(n0, CHUNK, "acc") for n0 in range(0, LEFT, CHUNK)]
-        for g in range(G2):
+        for g in range(G2 - 2):
             for sums in left:
                 passes2(sums, g, g + 1)
             if g == 2:
                 transpose_h(PAIRS - 1)
                 quantise_h(PAIRS - 1)
-        for sums in left:
-            activate2(sums)
-        for sums in left:
-            finish2(sums)
         halves = [open2(LEFT, CHUNK // 2, "side"), open2(LEFT + CHUNK // 2, CHUNK // 2, "acc")]
-        for g0 in (0, 2):
-            for sums in halves:
-                passes2(sums, g0, g0 + 2)
-        for sums in halves:
-            passes2(sums, 4, 6)
-        for sums in halves:
-            passes2(sums, 6, 8)
+        done = None
+        for sums in left + halves:
+            passes2(sums, G2 - 2 if sums in left else 0, G2)
             activate2(sums)
-        for sums in halves:
-            finish2(sums)
+            if done:
+                finish2(done)
+            done = sums
+        finish2(done)

@@ -69,7 +69,7 @@ def tile_node_interaction_w_kernel(
         nc.vector.memset(bias_rows[:].bitcast(I32), 0)
         nc.vector.memset(silu_seed[:], 0.0)
         nc.scalar.activation(out=silu_seed[:], in_=silu_seed[:], func=SILU)
-        nc.vector.memset(w1_planes[:, 0 : 2 * CHUNK].bitcast(I32), 0)
+        nc.vector.memset(w1_planes[:, 0 : 4 * CHUNK].bitcast(I32), 0)
         make_identity(nc, ident_f32[:])
         make_identity(nc, ident_bf16[:])
 
@@ -106,15 +106,15 @@ def tile_node_interaction_w_kernel(
         B1_ROWS = H // CHUNK
         B2_ROWS = D // CHUNK
         def load_bias(r0, rows, vector):
-            nc.gpsimd.dma_start(out=bias_rows[r0 : r0 + rows, :], in_=vector.rearrange("(r n) -> r n", n=CHUNK))
+            nc.sync.dma_start(out=bias_rows[r0 : r0 + rows, :], in_=vector.rearrange("(r n) -> r n", n=CHUNK))
 
-        load_bias(0, B1_ROWS, b1)
-        load_bias(B1_ROWS, B2_ROWS, b2)
         for k0 in (0, D // 2):
             for h, rows in enumerate((node_embed, ori)):
                 nc.sync.dma_start(out=x_rows[:, h, k0 : k0 + D // 2], in_=rows[:, k0 : k0 + D // 2])
+        load_bias(0, B1_ROWS, b1)
+        load_bias(B1_ROWS, B2_ROWS, b2)
         load_words(w1_words, w1_dram, 0, 1, 0, 2 * CHUNK)
-        load_scales1(nc.sync, I32, 0, 2 * CHUNK)
+        load_scales1(nc.sync, I32, 0, 4 * CHUNK)
         for g in range(1, G1):
             load_words(w1_words, w1_dram, g, g + 1, 0, 2 * CHUNK)
         for pair in range(1, PAIRS):
@@ -183,8 +183,8 @@ def tile_node_interaction_w_kernel(
                 quantise_x(g - 1)
                 quantise_x(g)
             if g == 1:
-                nc.vector.memset(w1_planes[:, 2 * CHUNK : H].bitcast(I32), 0)
-                load_scales1(nc.gpsimd, F32, 2 * CHUNK, H)
+                nc.vector.memset(w1_planes[:, 4 * CHUNK : H].bitcast(I32), 0)
+                load_scales1(nc.gpsimd, F32, 4 * CHUNK, H)
         biases(0, 2)
 
         sums1 = {}

@@ -22,13 +22,14 @@ PACK = 4
 K_PASS = P * PACK
 G1 = D // K_PASS
 G2 = H // K_PASS
+BLOCK = 32
 CHUNK = 512
 PAIRS = H // (2 * CHUNK)
 PLANES = 4
 
 LEFT = 3 * CHUNK
 
-WARM = 4
+WARM = 6
 
 FLOPS = 2 * (HALVES * E) * D * H * 2
 
@@ -60,7 +61,10 @@ def tile_node_interaction_w_kernel(
         h_planes = keep.tile([P, G2, HALVES * E], U8, align_bytes=64)
         bias_rows = keep.tile([P, CHUNK], BF16, align_bytes=64)
         idle = keep.tile([P, CHUNK], BF16, align_bytes=64)
-        bias_all = keep.tile([P, H + D], BF16)
+        bias_blocks = keep.tile([P, 2, BLOCK], F32, align_bytes=64)
+        bias_columns = keep.tile([P, 2, BLOCK], F32, align_bytes=64)
+        bias_wide = keep.tile([P, BLOCK, BLOCK], F32, align_bytes=64)
+        bias_all = keep.tile([P, H + D], BF16, align_bytes=64)
         silu_seed = keep.tile([P, 8], F32)
         ident_f32 = keep.tile([P, P], F32)
         ident_bf16 = keep.tile([P, P], BF16)
@@ -104,19 +108,28 @@ def tile_node_interaction_w_kernel(
                 load_words(w1_words, w1_dram, g, g + 1, 2 * CHUNK * pair, 2 * CHUNK * (pair + 1))
 
         B1_ROWS = H // CHUNK
-        B2_ROWS = D // CHUNK
+        def load_bias_blocks(queue, which, vector):
+            for quad in range(4):
+                queue.dma_start(
+                    out=bias_blocks[32 * quad : 32 * (quad + 1), which, :].bitcast(BF16),
+                    in_=vector.rearrange("(b i) -> b i", i=2 * BLOCK),
+                )
+
         def load_bias(r0, rows, vector):
             nc.sync.dma_start(out=bias_rows[r0 : r0 + rows, :], in_=vector.rearrange("(r n) -> r n", n=CHUNK))
 
-        for k0 in (0, D // 2):
+        def load_x(k0):
             for h, rows in enumerate((node_embed, ori)):
                 nc.sync.dma_start(out=x_rows[:, h, k0 : k0 + D // 2], in_=rows[:, k0 : k0 + D // 2])
+
+        load_x(0)
         load_bias(0, B1_ROWS, b1)
-        load_bias(B1_ROWS, B2_ROWS, b2)
         load_words(w1_words, w1_dram, 0, 1, 0, 2 * CHUNK)
-        load_scales1(nc.sync, I32, 0, 4 * CHUNK)
+        load_scales1(nc.sync, I32, 0, 2 * CHUNK)
+        load_x(D // 2)
         for g in range(1, G1):
             load_words(w1_words, w1_dram, g, g + 1, 0, 2 * CHUNK)
+        load_scales1(nc.sync, I32, 2 * CHUNK, 4 * CHUNK)
         for pair in range(1, PAIRS):
             load_gate(2 * CHUNK * (pair - 1), 2 * CHUNK * pair)
             load_pair1(pair)
@@ -136,7 +149,7 @@ def tile_node_interaction_w_kernel(
         spreads = {}
 
         def spread_bias(k):
-            spread = ring("acc" if k >= 4 else "side", [P, 2 * CHUNK], BF16, "spread_%d" % k)
+            spread = ring("side", [P, 2 * CHUNK], BF16, "spread_%d" % k)
             for j in range(2):
                 nc.tensor.matmul(
                     out=spread[:, CHUNK * j : CHUNK * (j + 1)],
@@ -149,6 +162,15 @@ def tile_node_interaction_w_kernel(
 
         def keep_bias(k):
             nc.scalar.copy(out=bias_all[:, 2 * CHUNK * k : 2 * CHUNK * (k + 1)], in_=spreads[k][:])
+
+        def spread_on_vector(which, n0):
+            nc.vector.transpose(bias_columns[:, which, :], bias_blocks[:, which, :])
+            nc.vector.tensor_copy(
+                out=bias_wide[:], in_=bias_columns[:, which, :].unsqueeze(2).to_broadcast([P, BLOCK, BLOCK])
+            )
+            nc.vector.transpose(
+                bias_all[:, n0 : n0 + D].bitcast(F32), bias_wide[:].rearrange("p b j -> p (b j)")
+            )
 
         def quantise_x(g):
             nc.vector.quantize_mx(
@@ -175,17 +197,18 @@ def tile_node_interaction_w_kernel(
                 spread_bias(k)
                 keep_bias(k)
 
-        for g in range(G1):
-            transpose_x(g)
-            copy = nc.vector.tensor_copy if g % 2 == 0 else nc.scalar.copy
-            copy(out=x_grouped[:, g].bitcast(F32), in_=x_t[g][:].rearrange("p h u r -> p h r u"))
-            if g % 2 == 1:
-                quantise_x(g - 1)
-                quantise_x(g)
-            if g == 1:
-                nc.vector.memset(w1_planes[:, 4 * CHUNK : H].bitcast(I32), 0)
-                load_scales1(nc.gpsimd, F32, 4 * CHUNK, H)
+        def take_x(g0):
+            for g in (g0, g0 + 1):
+                transpose_x(g)
+                copy = nc.vector.tensor_copy if g == g0 else nc.scalar.copy
+                copy(out=x_grouped[:, g].bitcast(F32), in_=x_t[g][:].rearrange("p h u r -> p h r u"))
+            quantise_x(g0)
+            quantise_x(g0 + 1)
+
+        take_x(0)
         biases(0, 2)
+        nc.vector.memset(w1_planes[:, 4 * CHUNK : H].bitcast(I32), 0)
+        load_scales1(nc.gpsimd, F32, 4 * CHUNK, H)
 
         sums1 = {}
         acts = {}
@@ -196,15 +219,16 @@ def tile_node_interaction_w_kernel(
         def by_pair(columns):
             return columns.rearrange("p (q u e) -> p u q e", u=2, e=2)
 
-        def passes1(pair):
-            chunks = (2 * pair, 2 * pair + 1)
-            for c in chunks:
+        def open1(pair):
+            for c in (2 * pair, 2 * pair + 1):
                 for h in range(HALVES):
                     sums1[(c, h)] = ring("acc", [P, CHUNK], F32, "sums1_%d_%d" % (c, h))
                 acts[c] = work.tile([P, HALVES, 2, E, 2], F32, tag="acts", bufs=4, name="acts_%d" % c)
                 h_sorted[c] = work.tile([P, HALVES, 2, E, 2], BF16, tag="h_sorted", bufs=4, name="h_sorted_%d" % c)
-            for g in range(G1):
-                for c in chunks:
+
+        def passes1(pair, g0, g1):
+            for g in range(g0, g1):
+                for c in (2 * pair, 2 * pair + 1):
                     for h in range(HALVES):
                         nc.tensor.matmul_mx(
                             out=sums1[(c, h)][:],
@@ -259,17 +283,22 @@ def tile_node_interaction_w_kernel(
                 )
 
         for pair in range(PAIRS):
-            passes1(pair)
+            open1(pair)
+            passes1(pair, 0, 1)
+            if pair == 0:
+                take_x(2)
+            passes1(pair, 1, G1)
             if pair >= 2:
                 quantise_h(pair - 2)
             if pair >= 1:
                 transpose_h(pair - 1)
             activate(pair)
             if pair == 0:
-                biases(2, 6)
+                biases(2, 4)
                 nc.vector.memset(w2_planes[:].rearrange("p a n -> p (a n)").bitcast(I32), 0)
                 for a in range(G2 // PLANES):
                     load_scales2(a)
+                load_bias_blocks(nc.gpsimd, 0, b2)
         quantise_h(PAIRS - 2)
 
         out_rows = out.rearrange("e a c -> e (a c)")
@@ -318,6 +347,7 @@ def tile_node_interaction_w_kernel(
             if g == 2:
                 transpose_h(PAIRS - 1)
                 quantise_h(PAIRS - 1)
+        spread_on_vector(0, H)
         halves = [open2(LEFT, CHUNK // 2, "side"), open2(LEFT + CHUNK // 2, CHUNK // 2, "acc")]
         done = None
         for sums in left + halves:

@@ -133,6 +133,7 @@ def tile_node_interaction_w_kernel(
         for pair in range(1, PAIRS):
             load_gate(2 * CHUNK * (pair - 1), 2 * CHUNK * pair)
             load_pair1(pair)
+        load_bias_blocks(nc.sync, 0, b2)
         load_gate(H - 2 * CHUNK, H)
         def load2(g0, g1, n0, n1):
             load_words(w2_words, w2_dram, g0, g1, n0, n1)
@@ -298,7 +299,6 @@ def tile_node_interaction_w_kernel(
                 nc.vector.memset(w2_planes[:].rearrange("p a n -> p (a n)").bitcast(I32), 0)
                 for a in range(G2 // PLANES):
                     load_scales2(a)
-                load_bias_blocks(nc.gpsimd, 0, b2)
         quantise_h(PAIRS - 2)
 
         out_rows = out.rearrange("e a c -> e (a c)")
@@ -341,7 +341,7 @@ def tile_node_interaction_w_kernel(
             nc.sync.dma_start(out=out_rows[:, n0 : n0 + width], in_=both[:, 0:width])
 
         left = [open2(n0, CHUNK, "acc") for n0 in range(0, LEFT, CHUNK)]
-        for g in range(G2 - 2):
+        for g in range(G2):
             for sums in left:
                 passes2(sums, g, g + 1)
             if g == 2:
@@ -350,10 +350,17 @@ def tile_node_interaction_w_kernel(
         spread_on_vector(0, H)
         halves = [open2(LEFT, CHUNK // 2, "side"), open2(LEFT + CHUNK // 2, CHUNK // 2, "acc")]
         done = None
-        for sums in left + halves:
-            passes2(sums, G2 - 2 if sums in left else 0, G2)
+        for sums in left:
             activate2(sums)
             if done:
                 finish2(done)
+            done = sums
+        for g0 in (0, 2, 4):
+            for sums in halves:
+                passes2(sums, g0, g0 + 2)
+        for sums in halves:
+            passes2(sums, 6, 8)
+            activate2(sums)
+            finish2(done)
             done = sums
         finish2(done)

@@ -210,6 +210,9 @@ def tile_node_interaction_w_kernel(
         biases(0, 2)
         nc.vector.memset(w1_planes[:, 4 * CHUNK : H].bitcast(I32), 0)
         load_scales1(nc.gpsimd, F32, 4 * CHUNK, H)
+        nc.vector.memset(w2_planes[:].rearrange("p a n -> p (a n)").bitcast(I32), 0)
+        for a in range(G2 // PLANES):
+            load_scales2(a)
 
         sums1 = {}
         acts = {}
@@ -296,9 +299,6 @@ def tile_node_interaction_w_kernel(
             activate(pair)
             if pair == 0:
                 biases(2, 4)
-                nc.vector.memset(w2_planes[:].rearrange("p a n -> p (a n)").bitcast(I32), 0)
-                for a in range(G2 // PLANES):
-                    load_scales2(a)
         quantise_h(PAIRS - 2)
 
         out_rows = out.rearrange("e a c -> e (a c)")

@@ -332,12 +332,12 @@ def tile_node_interaction_w_kernel(
                 )
                 nc.scalar.activation(out=y[:, h, 0:width], in_=y[:, h, 0:width], func=SILU)
 
-        def finish2(sums):
+        def finish2(sums, engine):
             n0 = sums[0][2]
             width = sums[0][0].shape[1]
             y = ys[n0]
             both = work.tile([P, CHUNK], F32, tag="both", bufs=5, name="both_%d" % n0)
-            nc.vector.tensor_tensor(out=both[:, 0:width], in0=y[:, 0, 0:width], in1=y[:, 1, 0:width], op=ADD)
+            engine.tensor_tensor(out=both[:, 0:width], in0=y[:, 0, 0:width], in1=y[:, 1, 0:width], op=ADD)
             nc.sync.dma_start(out=out_rows[:, n0 : n0 + width], in_=both[:, 0:width])
 
         left = [open2(n0, CHUNK, "acc") for n0 in range(0, LEFT, CHUNK)]
@@ -349,18 +349,15 @@ def tile_node_interaction_w_kernel(
                 quantise_h(PAIRS - 1)
         spread_on_vector(0, H)
         halves = [open2(LEFT, CHUNK // 2, "side"), open2(LEFT + CHUNK // 2, CHUNK // 2, "acc")]
-        done = None
         for sums in left:
             activate2(sums)
-            if done:
-                finish2(done)
-            done = sums
+        for sums in left:
+            finish2(sums, nc.gpsimd)
         for g0 in (0, 2, 4):
             for sums in halves:
                 passes2(sums, g0, g0 + 2)
         for sums in halves:
             passes2(sums, 6, 8)
             activate2(sums)
-            finish2(done)
-            done = sums
-        finish2(done)
+        for sums in halves:
+            finish2(sums, nc.vector)

@@ -134,13 +134,14 @@ def tile_node_interaction_w_kernel(
             load_gate(2 * CHUNK * (pair - 1), 2 * CHUNK * pair)
             load_pair1(pair)
         load_bias_blocks(nc.sync, 0, b2)
-        load_gate(H - 2 * CHUNK, H)
         def load2(g0, g1, n0, n1):
             load_words(w2_words, w2_dram, g0, g1, n0, n1)
 
         for a in range(G2 // PLANES):
             for g in range(PLANES * a, PLANES * (a + 1)):
                 load2(g, g + 1, 0, LEFT)
+                if g == 0:
+                    load_gate(H - 2 * CHUNK, H)
         for g in (0, 2):
             load2(g, g + 2, LEFT, D)
         load2(4, 6, LEFT, D)
@@ -303,41 +304,43 @@ def tile_node_interaction_w_kernel(
 
         out_rows = out.rearrange("e a c -> e (a c)")
 
-        def open2(n0, width, tag):
-            return [(ring(tag, [P, width], F32, "sums2_%d_%d" % (n0, h)), h, n0) for h in range(HALVES)]
+        def open2(n0, width, tag, last_parts=1):
+            block = {"n0": n0, "width": width, "sums": []}
+            for h in range(HALVES):
+                part = width // (last_parts if h == HALVES - 1 else 1)
+                for n in range(n0, n0 + width, part):
+                    acc = ring(tag, [P, part], F32, "sums2_%d_%d" % (n, h))
+                    block["sums"].append((acc, h, n, part))
+            block["y"] = work.tile([P, HALVES, CHUNK], F32, tag="acts", bufs=4, name="y_%d" % n0)
+            return block
 
-        def passes2(sums, g0, g1):
-            for acc, h, n0 in sums:
-                width = acc.shape[1]
+        def passes2(block, g0, g1):
+            for acc, h, n, part in block["sums"]:
                 for g in range(g0, g1):
                     nc.tensor.matmul_mx(
                         out=acc[:],
                         lhsT=h_words[:, g, E * h : E * (h + 1)].bitcast(FP8X4),
                         lhsT_scale=h_planes[:, g, E * h : E * (h + 1)],
-                        rhs=w2_words[:, g, n0 : n0 + width].bitcast(FP8X4),
-                        rhs_scale=w2_planes[4 * (g % PLANES) : P, g // PLANES, n0 : n0 + width],
+                        rhs=w2_words[:, g, n : n + part].bitcast(FP8X4),
+                        rhs_scale=w2_planes[4 * (g % PLANES) : P, g // PLANES, n : n + part],
                         start=(g == 0),
                         stop=(g == G2 - 1),
                     )
 
-        ys = {}
+        def activate2(block):
+            for acc, h, n, part in block["sums"]:
+                y = block["y"][:, h, n - block["n0"] : n - block["n0"] + part]
+                nc.vector.tensor_tensor(out=y, in0=acc[:], in1=bias_all[:, H + n : H + n + part], op=ADD)
+                nc.scalar.activation(out=y, in_=y, func=SILU)
 
-        def activate2(sums):
-            n0 = sums[0][2]
-            width = sums[0][0].shape[1]
-            ys[n0] = y = work.tile([P, HALVES, CHUNK], F32, tag="acts", bufs=4, name="y_%d" % n0)
-            for acc, h, n0_same in sums:
-                nc.vector.tensor_tensor(
-                    out=y[:, h, 0:width], in0=acc[:], in1=bias_all[:, H + n0 : H + n0 + width], op=ADD
+        def finish2(block, engine):
+            both = work.tile([P, CHUNK], F32, tag="both", bufs=5, name="both_%d" % block["n0"])
+            n0, width = block["n0"], block["width"]
+            part = block["sums"][-1][3]
+            for c in range(0, width, part):
+                engine.tensor_tensor(
+                    out=both[:, c : c + part], in0=block["y"][:, 0, c : c + part], in1=block["y"][:, 1, c : c + part], op=ADD
                 )
-                nc.scalar.activation(out=y[:, h, 0:width], in_=y[:, h, 0:width], func=SILU)
-
-        def finish2(sums, engine):
-            n0 = sums[0][2]
-            width = sums[0][0].shape[1]
-            y = ys[n0]
-            both = work.tile([P, CHUNK], F32, tag="both", bufs=5, name="both_%d" % n0)
-            engine.tensor_tensor(out=both[:, 0:width], in0=y[:, 0, 0:width], in1=y[:, 1, 0:width], op=ADD)
             nc.sync.dma_start(out=out_rows[:, n0 : n0 + width], in_=both[:, 0:width])
 
         left = [open2(n0, CHUNK, "acc") for n0 in range(0, LEFT, CHUNK)]
@@ -348,16 +351,16 @@ def tile_node_interaction_w_kernel(
                 transpose_h(PAIRS - 1)
                 quantise_h(PAIRS - 1)
         spread_on_vector(0, H)
-        halves = [open2(LEFT, CHUNK // 2, "side"), open2(LEFT + CHUNK // 2, CHUNK // 2, "acc")]
+        halves = [open2(LEFT, CHUNK // 2, "side"), open2(LEFT + CHUNK // 2, CHUNK // 2, "acc", 2)]
         for sums in left:
             activate2(sums)
         for sums in left:
             finish2(sums, nc.gpsimd)
-        for g0 in (0, 2, 4):
+        for g0 in (0, 2):
             for sums in halves:
                 passes2(sums, g0, g0 + 2)
         for sums in halves:
-            passes2(sums, 6, 8)
+            passes2(sums, 4, 8)
             activate2(sums)
         for sums in halves:
             finish2(sums, nc.vector)

from contextlib import ExitStack

import concourse.mybir as mybir
from concourse.masks import make_identity

F32 = mybir.dt.float32
BF16 = mybir.dt.bfloat16
I32 = mybir.dt.int32
U32 = mybir.dt.uint32
U8 = mybir.dt.uint8
FP8X4 = mybir.dt.float8_e4m3fn_x4
SILU = mybir.ActivationFunctionType.Silu
ADD = mybir.AluOpType.add
MULT = mybir.AluOpType.mult

P = 128
E = 128
HALVES = 2
D = 2048
H = 4096
PACK = 4
K_PASS = P * PACK
G1 = D // K_PASS
G2 = H // K_PASS
BLOCK = 32
CHUNK = 512
PAIRS = H // (2 * CHUNK)
PLANES = 4

LEFT = 3 * CHUNK

WARM = 6

FLOPS = 2 * (HALVES * E) * D * H * 2


def tile_node_interaction_w_kernel(
    tc, node_embed, x_edge_c, ori, W1_words, W1_scales, b1, W2_words, W2_scales, b2, edge_num, out
):
    nc = tc.nc
    assert edge_num == E
    with ExitStack() as ctx:
        ctx.enter_context(tc.manual_schedule())
        keep = ctx.enter_context(tc.tile_pool(name="keep", bufs=1))
        work = ctx.enter_context(tc.tile_pool(name="work", bufs=2))
        psum = ctx.enter_context(tc.psum_pool(name="psum", bufs=1))

        def ring(tag, shape, dtype, name):
            return psum.tile(shape, dtype, tag=tag, bufs={"acc": 6, "side": 2}[tag], name=name)

        w1_words = keep.tile([P, G1, H], U32, align_bytes=64)
        w2_words = keep.tile([P, G2, D], U32, align_bytes=64)
        w1_planes = keep.tile([P, H], U8, align_bytes=64)
        w2_planes = keep.tile([P, G2 // PLANES, D], U8, align_bytes=64)
        x_rows = keep.tile([P, HALVES, D], BF16, align_bytes=64)
        gate = keep.tile([P, H], BF16, align_bytes=64)
        x_grouped = keep.tile([P, G1, HALVES, E, PACK], BF16, align_bytes=64)
        x_words = keep.tile([P, G1, HALVES * E], U32, align_bytes=64)
        x_planes = keep.tile([P, G1, HALVES * E], U8, align_bytes=64)
        h_words = keep.tile([P, G2, HALVES * E], U32, align_bytes=64)
        h_planes = keep.tile([P, G2, HALVES * E], U8, align_bytes=64)
        bias_rows = keep.tile([P, CHUNK], BF16, align_bytes=64)
        idle = keep.tile([P, CHUNK], BF16, align_bytes=64)
        bias_blocks = keep.tile([P, 2, BLOCK], F32, align_bytes=64)
        bias_columns = keep.tile([P, 2, BLOCK], F32, align_bytes=64)
        bias_wide = keep.tile([P, BLOCK, BLOCK], F32, align_bytes=64)
        bias_all = keep.tile([P, H + D], BF16, align_bytes=64)
        silu_seed = keep.tile([P, 8], F32)
        ident_f32 = keep.tile([P, P], F32)
        ident_bf16 = keep.tile([P, P], BF16)

        nc.vector.memset(idle[:].bitcast(I32), 0)
        nc.vector.memset(bias_rows[:].bitcast(I32), 0)
        nc.vector.memset(silu_seed[:], 0.0)
        nc.scalar.activation(out=silu_seed[:], in_=silu_seed[:], func=SILU)
        nc.vector.memset(w1_planes[:, 0 : 4 * CHUNK].bitcast(I32), 0)
        make_identity(nc, ident_f32[:])
        make_identity(nc, ident_bf16[:])

        w1_dram = W1_words.rearrange("g p n t -> g p (n t)").bitcast(I32)
        w2_dram = W2_words.rearrange("g p n t -> g p (n t)").bitcast(I32)

        def load_words(sbuf, dram, g0, g1, n0, n1):
            nc.sync.dma_start(
                out=sbuf[:, g0:g1, n0:n1].bitcast(I32),
                in_=dram[g0:g1, :, n0:n1].rearrange("g p n -> p g n"),
            )

        def load_scales1(queue, words, n0, n1):
            for quad in range(4):
                queue.dma_start(
                    out=w1_planes[32 * quad : 32 * quad + 16, n0:n1].bitcast(words),
                    in_=W1_scales.bitcast(words)[:, 4 * quad : 4 * quad + 4, n0 // PACK : n1 // PACK],
                )

        def load_gate(n0, n1):
            nc.sync.dma_start(out=gate[:, n0:n1], in_=x_edge_c[:, n0:n1])

        def load_scales2(a):
            for quad in range(4):
                nc.gpsimd.dma_start(
                    out=w2_planes[32 * quad : 32 * quad + 16, a, :].bitcast(F32),
                    in_=W2_scales.bitcast(F32)[PLANES * a : PLANES * (a + 1), 4 * quad : 4 * quad + 4, :],
                )

        def load_pair1(pair):
            for g in range(G1):
                load_words(w1_words, w1_dram, g, g + 1, 2 * CHUNK * pair, 2 * CHUNK * (pair + 1))

        B1_ROWS = H // CHUNK
        def load_bias_blocks(queue, which, vector):
            for quad in range(4):
                queue.dma_start(
                    out=bias_blocks[32 * quad : 32 * (quad + 1), which, :].bitcast(BF16),
                    in_=vector.rearrange("(b i) -> b i", i=2 * BLOCK),
                )

        def load_bias(r0, rows, vector):
            nc.sync.dma_start(out=bias_rows[r0 : r0 + rows, :], in_=vector.rearrange("(r n) -> r n", n=CHUNK))

        def load_x(k0):
            for h, rows in enumerate((node_embed, ori)):
                nc.sync.dma_start(out=x_rows[:, h, k0 : k0 + D // 2], in_=rows[:, k0 : k0 + D // 2])

        load_x(0)
        load_bias(0, B1_ROWS, b1)
        load_words(w1_words, w1_dram, 0, 1, 0, 2 * CHUNK)
        load_scales1(nc.sync, I32, 0, 2 * CHUNK)
        load_x(D // 2)
        for g in range(1, G1):
            load_words(w1_words, w1_dram, g, g + 1, 0, 2 * CHUNK)
        load_scales1(nc.sync, I32, 2 * CHUNK, 4 * CHUNK)
        for pair in range(1, PAIRS):
            load_gate(2 * CHUNK * (pair - 1), 2 * CHUNK * pair)
            load_pair1(pair)
        load_bias_blocks(nc.sync, 0, b2)
        def load2(g0, g1, n0, n1):
            load_words(w2_words, w2_dram, g0, g1, n0, n1)

        for a in range(G2 // PLANES):
            for g in range(PLANES * a, PLANES * (a + 1)):
                load2(g, g + 1, 0, LEFT)
                if g == 0:
                    load_gate(H - 2 * CHUNK, H)
        for g in (0, 2):
            load2(g, g + 2, LEFT, D)
        load2(4, 6, LEFT, D)
        for n0 in (LEFT, LEFT + CHUNK // 2):
            load2(6, 8, n0, n0 + CHUNK // 2)

        spreads = {}

        def spread_bias(k):
            spread = ring("side", [P, 2 * CHUNK], BF16, "spread_%d" % k)
            for j in range(2):
                nc.tensor.matmul(
                    out=spread[:, CHUNK * j : CHUNK * (j + 1)],
                    lhsT=ident_bf16[:, 2 * k + j : 2 * k + j + 1].to_broadcast([P, P]),
                    rhs=bias_rows[:],
                    start=True,
                    stop=True,
                )
            spreads[k] = spread

        def keep_bias(k):
            nc.scalar.copy(out=bias_all[:, 2 * CHUNK * k : 2 * CHUNK * (k + 1)], in_=spreads[k][:])

        def spread_on_vector(which, n0):
            nc.vector.transpose(bias_columns[:, which, :], bias_blocks[:, which, :])
            nc.vector.tensor_copy(
                out=bias_wide[:], in_=bias_columns[:, which, :].unsqueeze(2).to_broadcast([P, BLOCK, BLOCK])
            )
            nc.vector.transpose(
                bias_all[:, n0 : n0 + D].bitcast(F32), bias_wide[:].rearrange("p b j -> p (b j)")
            )

        def quantise_x(g):
            nc.vector.quantize_mx(
                out=x_words[:, g, :].bitcast(FP8X4),
                scales=x_planes[:, g, :],
                in_=x_grouped[:, g].rearrange("p h r t -> p (h r t)"),
            )

        x_t = [ring("acc", [P, HALVES, 2, E], F32, "x_t_%d" % g) for g in range(G1)]

        def transpose_x(g):
            for h in range(HALVES):
                pairs_of_k = x_rows[:, h, :].bitcast(F32)
                for u in range(2):
                    nc.tensor.transpose(
                        x_t[g][:, h, u, :], pairs_of_k[:, 256 * g + u : 256 * (g + 1) : 2], ident_f32[:]
                    )

        warm = ring("side", [P, CHUNK], F32, "warm")
        for k in range(WARM):
            nc.tensor.matmul(out=warm[:], lhsT=idle[:, 0:P], rhs=idle[:], start=True, stop=True)
        def biases(k0, k1):
            for k in range(k0, k1):
                spread_bias(k)
                keep_bias(k)

        def take_x(g0):
            for g in (g0, g0 + 1):
                transpose_x(g)
                copy = nc.vector.tensor_copy if g == g0 else nc.scalar.copy
                copy(out=x_grouped[:, g].bitcast(F32), in_=x_t[g][:].rearrange("p h u r -> p h r u"))
            quantise_x(g0)
            quantise_x(g0 + 1)

        take_x(0)
        biases(0, 2)
        nc.vector.memset(w1_planes[:, 4 * CHUNK : H].bitcast(I32), 0)
        load_scales1(nc.gpsimd, F32, 4 * CHUNK, H)
        nc.vector.memset(w2_planes[:].rearrange("p a n -> p (a n)").bitcast(I32), 0)
        for a in range(G2 // PLANES):
            load_scales2(a)

        sums1 = {}
        acts = {}
        h_sorted = {}
        h_t = {}
        h_grouped = {}

        def by_pair(columns):
            return columns.rearrange("p (q u e) -> p u q e", u=2, e=2)

        def open1(pair):
            for c in (2 * pair, 2 * pair + 1):
                for h in range(HALVES):
                    sums1[(c, h)] = ring("acc", [P, CHUNK], F32, "sums1_%d_%d" % (c, h))
                acts[c] = work.tile([P, HALVES, 2, E, 2], F32, tag="acts", bufs=4, name="acts_%d" % c)
                h_sorted[c] = work.tile([P, HALVES, 2, E, 2], BF16, tag="h_sorted", bufs=4, name="h_sorted_%d" % c)

        def passes1(pair, g0, g1):
            for g in range(g0, g1):
                for c in (2 * pair, 2 * pair + 1):
                    for h in range(HALVES):
                        nc.tensor.matmul_mx(
                            out=sums1[(c, h)][:],
                            lhsT=x_words[:, g, E * h : E * (h + 1)].bitcast(FP8X4),
                            lhsT_scale=x_planes[:, g, E * h : E * (h + 1)],
                            rhs=w1_words[:, g, CHUNK * c : CHUNK * (c + 1)].bitcast(FP8X4),
                            rhs_scale=w1_planes[4 * g : P, CHUNK * c : CHUNK * (c + 1)],
                            start=(g == 0),
                            stop=(g == G1 - 1),
                        )

        def activate(pair):
            chunks = (2 * pair, 2 * pair + 1)
            for c in chunks:
                for h in range(HALVES):
                    nc.vector.tensor_tensor(
                        out=acts[c][:, h],
                        in0=by_pair(sums1[(c, h)][:]),
                        in1=by_pair(bias_all[:, CHUNK * c : CHUNK * (c + 1)]),
                        op=ADD,
                    )
            for c in chunks:
                for h in range(HALVES):
                    nc.scalar.activation(out=acts[c][:, h], in_=acts[c][:, h], func=SILU)
            for c in chunks:
                for h in range(HALVES):
                    nc.vector.tensor_tensor(
                        out=h_sorted[c][:, h],
                        in0=acts[c][:, h],
                        in1=by_pair(gate[:, CHUNK * c : CHUNK * (c + 1)]),
                        op=MULT,
                    )

        def transpose_h(pair):
            for c in (2 * pair, 2 * pair + 1):
                h_t[c] = ring("side", [P, HALVES, 2, E], F32, "h_t_%d" % c)
                for h in range(HALVES):
                    for u in range(2):
                        pairs_of_k = h_sorted[c][:, h, u].rearrange("p q e -> p (q e)").bitcast(F32)
                        nc.tensor.transpose(h_t[c][:, h, u, :], pairs_of_k, ident_f32[:])

        def quantise_h(pair):
            chunks = (2 * pair, 2 * pair + 1)
            for c in chunks:
                h_grouped[c] = work.tile([P, HALVES, E, PACK], BF16, tag="h_grouped", name="h_grouped_%d" % c, align_bytes=64)
                nc.scalar.copy(out=h_grouped[c][:].bitcast(F32), in_=h_t[c][:].rearrange("p h u r -> p h r u"))
            for c in chunks:
                nc.vector.quantize_mx(
                    out=h_words[:, c, :].bitcast(FP8X4),
                    scales=h_planes[:, c, :],
                    in_=h_grouped[c][:].rearrange("p h r t -> p (h r t)"),
                )

        for pair in range(PAIRS):
            open1(pair)
            passes1(pair, 0, 1)
            if pair == 0:
                take_x(2)
            passes1(pair, 1, G1)
            if pair >= 2:
                quantise_h(pair - 2)
            if pair >= 1:
                transpose_h(pair - 1)
            activate(pair)
            if pair == 0:
                biases(2, 4)
        quantise_h(PAIRS - 2)

        out_rows = out.rearrange("e a c -> e (a c)")

        def open2(n0, width, tag, last_parts=1):
            block = {"n0": n0, "width": width, "sums": []}
            for h in range(HALVES):
                part = width // (last_parts if h == HALVES - 1 else 1)
                for n in range(n0, n0 + width, part):
                    acc = ring(tag, [P, part], F32, "sums2_%d_%d" % (n, h))
                    block["sums"].append((acc, h, n, part))
            block["y"] = work.tile([P, HALVES, CHUNK], F32, tag="acts", bufs=4, name="y_%d" % n0)
            return block

        def passes2(block, g0, g1):
            for acc, h, n, part in block["sums"]:
                for g in range(g0, g1):
                    nc.tensor.matmul_mx(
                        out=acc[:],
                        lhsT=h_words[:, g, E * h : E * (h + 1)].bitcast(FP8X4),
                        lhsT_scale=h_planes[:, g, E * h : E * (h + 1)],
                        rhs=w2_words[:, g, n : n + part].bitcast(FP8X4),
                        rhs_scale=w2_planes[4 * (g % PLANES) : P, g // PLANES, n : n + part],
                        start=(g == 0),
                        stop=(g == G2 - 1),
                    )

        def activate2(block):
            for acc, h, n, part in block["sums"]:
                y = block["y"][:, h, n - block["n0"] : n - block["n0"] + part]
                nc.vector.tensor_tensor(out=y, in0=acc[:], in1=bias_all[:, H + n : H + n + part], op=ADD)
                nc.scalar.activation(out=y, in_=y, func=SILU)

        def finish2(block, engine):
            both = work.tile([P, CHUNK], F32, tag="both", bufs=5, name="both_%d" % block["n0"])
            n0, width = block["n0"], block["width"]
            part = block["sums"][-1][3]
            for c in range(0, width, part):
                engine.tensor_tensor(
                    out=both[:, c : c + part], in0=block["y"][:, 0, c : c + part], in1=block["y"][:, 1, c : c + part], op=ADD
                )
            nc.sync.dma_start(out=out_rows[:, n0 : n0 + width], in_=both[:, 0:width])

        left = [open2(n0, CHUNK, "acc") for n0 in range(0, LEFT, CHUNK)]
        for g in range(G2):
            for sums in left:
                passes2(sums, g, g + 1)
            if g == 2:
                transpose_h(PAIRS - 1)
                quantise_h(PAIRS - 1)
        spread_on_vector(0, H)
        halves = [open2(LEFT, CHUNK // 2, "side"), open2(LEFT + CHUNK // 2, CHUNK // 2, "acc", 2)]
        for sums in left:
            activate2(sums)
        for sums in left:
            finish2(sums, nc.gpsimd)
        for g0 in (0, 2):
            for sums in halves:
                passes2(sums, g0, g0 + 2)
        for sums in halves:
            passes2(sums, 4, 8)
            activate2(sums)
        for sums in halves:
            finish2(sums, nc.vector)
